import numpy as np
import ml_dtypes


def mxq(x, axis, fmt="e4m3"):
    dtype, down = {"e4m3": (ml_dtypes.float8_e4m3fn, 7), "e5m2": (ml_dtypes.float8_e5m2, 14)}[fmt]
    v = np.moveaxis(np.asarray(x, np.float32).astype(ml_dtypes.bfloat16).astype(np.float64), axis, -1)
    blocks = v.reshape(v.shape[:-1] + (-1, 32))
    amax = np.abs(blocks).max(-1, keepdims=True)
    byte = np.maximum(np.where(amax > 0, np.frexp(amax)[1] - 1 + 127, 0) - down, 1)
    scale = np.exp2(byte - 127.0)
    codes = (blocks / scale).astype(np.float32).astype(dtype).astype(np.float64)
    return np.moveaxis((codes * scale).reshape(v.shape), -1, axis)


WIDE = False


def mx_kscale(k):
    if not WIDE:
        return np.ones(k)
    levels = np.array([10, -10, 5, -5, 0])
    if k % 512:
        return np.exp2(np.random.permutation(np.resize(levels, k // 32))).repeat(32)
    a = np.empty((k // 512, 16))
    for p in range(k // 512):
        a[p, :8] = np.random.permutation(np.resize(levels, 8))
        for g in range(8):
            far = levels[np.abs(levels - a[p, g]) >= 10]
            a[p, g + 8] = far[np.random.randint(len(far))]
    return np.exp2(a.ravel()).repeat(32)


BF16 = ml_dtypes.bfloat16


def bf(x):
    return np.asarray(x, np.float32).astype(BF16)


def f64(x):
    return np.asarray(x).astype(np.float64)


B, D_IN, H, D_OUT = 8192, 4096, 512, 128
H2 = 2 * H
LN_EPS = 1e-5


def draw0():
    s = mx_kscale(H)
    t = mx_kscale(H2)
    return {
        "h1": bf(np.tanh(np.random.standard_normal((B, H))) * s),
        "W_ih1": bf(np.random.standard_normal((H, H)) / np.sqrt(H) / s[None, :]),
        "b_ih1": bf(0.25 + 0.3 * np.random.standard_normal(H)),
        "b_hh1": bf(0.3 * np.random.standard_normal(H)),
        "ln_g": bf((1.0 + 0.1 * np.random.standard_normal(H2)) * t),
        "ln_b": bf(0.2 * np.random.standard_normal(H2) * t),
        "fc_W": bf(np.random.standard_normal((D_OUT, H2)) / np.sqrt(H2) / t[None, :]),
        "fc_b": bf(0.3 * np.random.standard_normal(D_OUT)),
    }


def core(h1, W_ih1, b_ih1, b_hh1, ln_g, ln_b, fc_W, fc_b):
    h2 = np.tanh((mxq(f64(h1), 1, "e4m3") @ mxq(f64(W_ih1), 1, "e4m3").T) + f64(b_ih1) + f64(b_hh1))
    combined = np.concatenate([h2, h2], axis=1)
    mu = combined.mean(axis=-1, keepdims=True)
    var = combined.var(axis=-1, keepdims=True)
    normed = (combined - mu) / np.sqrt(var + LN_EPS) * f64(ln_g) + f64(ln_b)
    return (mxq(normed, 1, "e4m3") @ mxq(f64(fc_W), 1, "e4m3").T) + f64(fc_b)


def e4m3fn_bytes(y):
    return np.clip(np.asarray(y, np.float64), -448.0, 448.0).astype(np.float32).astype(ml_dtypes.float8_e4m3fn).view(np.uint8)


def e4m3fn_values(b):
    return np.asarray(b, np.uint8).view(ml_dtypes.float8_e4m3fn).astype(np.float64)


def setup_inputs():
    d = draw0()
    x0 = np.asarray(d['h1']).astype(np.float64)
    s = (np.max(np.abs(x0), axis=(0,), keepdims=True) / 448.0).astype(np.float32)
    out = {}
    for k, v in d.items():
        if k == 'h1':
            out['h1_bytes'] = e4m3fn_bytes(x0 / s.astype(np.float64))
            out['h1_scale'] = s
        else:
            out[k] = v
    return out


def reference(h1_bytes, h1_scale, W_ih1, b_ih1, b_hh1, ln_g, ln_b, fc_W, fc_b):
    return core(e4m3fn_values(h1_bytes) * h1_scale.astype(np.float64), W_ih1, b_ih1, b_hh1, ln_g, ln_b, fc_W, fc_b)

@@ -1,0 +1,337 @@
+from contextlib import ExitStack
+
+import concourse.mybir as mybir
+from concourse.masks import make_identity
+
+B, H, H2, D_OUT = 8192, 512, 1024, 128
+P = 128
+T = 4
+EPS = 1e-5
+FLOPS = 2 * B * H * H + 2 * B * H2 * D_OUT
+SIZES = [2] + [4] * 15 + [2]
+
+F32 = mybir.dt.float32
+BF16 = mybir.dt.bfloat16
+U32 = mybir.dt.uint32
+U8 = mybir.dt.uint8
+FP8 = mybir.dt.float8_e4m3fn
+FP8X4 = mybir.dt.float8_e4m3fn_x4
+ACT = mybir.ActivationFunctionType
+ALU = mybir.AluOpType
+
+
+def tile_rnnclassifier_pa_t_kernel(tc, h1_bytes, h1_scale, W_ih1, b_ih1, b_hh1, ln_g, ln_b, fc_W, fc_b, out):
+    nc = tc.nc
+    first = [sum(SIZES[:c]) * P for c in range(len(SIZES))]
+    nch = len(SIZES)
+
+    def rows(ap, c):
+        n = SIZES[c]
+        return ap[first[c] : first[c] + n * P, :].rearrange("(q j) k -> q j k", j=n)
+
+    with ExitStack() as ctx:
+        const = ctx.enter_context(tc.tile_pool(name="const", bufs=1))
+        work = ctx.enter_context(tc.tile_pool(name="work", bufs=2))
+        stat = ctx.enter_context(tc.tile_pool(name="stat", bufs=4))
+        ps_a = ctx.enter_context(tc.psum_pool(name="ps_a", bufs=2))
+        ps_s = ctx.enter_context(tc.psum_pool(name="ps_s", bufs=3))
+        ps_f = ctx.enter_context(tc.psum_pool(name="ps_f", bufs=3))
+
+        xb, hx, xg, xc, xs = {}, {}, {}, {}, {}
+        hb, hh, zz, sm, nm, sq, rs, nb = {}, {}, {}, {}, {}, {}, {}, {}
+        mv = {}
+        yy, yg, yc, ys = {}, {}, {}, {}
+        osb, fmb, xtb, s1b, ob = {}, {}, {}, {}, {}
+
+        def load(c):
+            xb[c] = work.tile([P, 4, H], U8, name="x_bytes", align_bytes=64, bufs=6)
+            nc.sync.dma_start(out=xb[c][:, : SIZES[c], :], in_=rows(h1_bytes, c))
+
+        row_b = const.tile([P, H], BF16)
+        nc.vector.memset(row_b[:], 0.0)
+        row_f = const.tile([P, D_OUT], BF16)
+        nc.vector.memset(row_f[:], 0.0)
+        ones = const.tile([P, P], BF16)
+        nc.vector.memset(ones[:], 1.0)
+        ident = const.tile([P, P], F32)
+        make_identity(nc, ident[:])
+        half = const.tile([P, 4], F32)
+        nc.gpsimd.memset(half[:], -0.5)
+        dummy = const.tile([P, 1], F32)
+        nc.gpsimd.memset(dummy[:], 0.0)
+
+        load(0)
+        scale = const.tile([P, 2, H], F32)
+        nc.sync.dma_start(out=scale[:, 0, :], in_=h1_scale.rearrange("o k -> (o k)").partition_broadcast(P))
+        w_sb = const.tile([P, T, H], BF16)
+        nc.sync.dma_start(out=w_sb[:], in_=W_ih1.rearrange("(m t) k -> m t k", t=T))
+        nc.scalar.dma_start(out=row_b[0:1, :], in_=b_ih1.rearrange("(o k) -> o k", o=1))
+        nc.scalar.dma_start(out=row_b[1:2, :], in_=b_hh1.rearrange("(o k) -> o k", o=1))
+        load(1)
+        f_sb = const.tile([P, H2], BF16)
+        nc.sync.dma_start(out=f_sb[:], in_=fc_W)
+        g_raw = const.tile([P, 2, T], BF16)
+        nc.gpsimd.dma_start(out=g_raw[:], in_=ln_g.rearrange("(o p t) -> p o t", o=2, t=T))
+        b_raw = const.tile([P, 2, T], BF16)
+        nc.gpsimd.dma_start(out=b_raw[:], in_=ln_b.rearrange("(o p t) -> p o t", o=2, t=T))
+        nc.gpsimd.dma_start(out=row_f[0:1, :], in_=fc_b.rearrange("(o k) -> o k", o=1))
+        nc.scalar.activation(out=dummy[:], in_=dummy[:], func=ACT.Tanh)
+        nc.scalar.copy(out=scale[:, 1, :], in_=scale[:, 0, :])
+        bias = const.tile([P, H], F32)
+        g_col = const.tile([P, 2, T], F32)
+        b_col = const.tile([P, 2, T], F32)
+        fcb = const.tile([P, 4, D_OUT], F32)
+
+        w_grp = const.tile([P, H, T], BF16, align_bytes=64)
+        w_codes = const.tile([P, H], U32, align_bytes=64)
+        w_scales = const.tile([P, H], U8, align_bytes=64)
+        f_grp = const.tile([P, 2 * D_OUT, T], BF16, align_bytes=64)
+        f_codes = const.tile([P, 2 * D_OUT], U32, align_bytes=64)
+        f_scales = const.tile([P, 2 * D_OUT], U8, align_bytes=64)
+
+        def words(ap):
+            return ap.bitcast(F32)
+
+        def a1(c, h):
+            if c not in hx:
+                hx[c] = work.tile([P, 4, H], BF16, name="hx", align_bytes=64, bufs=3)
+            n = min(2, SIZES[c] - 2 * h)
+            dst = hx[c][:, 2 * h : 2 * h + n, :].rearrange("p j k -> p (j k)")
+            code = xb[c][:, 2 * h : 2 * h + n, :].rearrange("p j k -> p (j k)").bitcast(FP8)
+            if c == 0:
+                for j in range(2 * h, 2 * h + n):
+                    nc.vector.tensor_tensor(out=hx[c][:, j, :], in0=xb[c][:, j, :].bitcast(FP8), in1=scale[:, 0, :], op=ALU.mult)
+                return
+            nc.vector.tensor_tensor(out=dst, in0=code, in1=scale[:, :n, :].rearrange("p a k -> p (a k)"), op=ALU.mult)
+
+        def a2p(c, h):
+            n = min(2, SIZES[c] - 2 * h)
+            xtb[c, h] = ps_a.tile([P, 2, 2, P], F32, name="xt")
+            for jj in range(n):
+                w = words(hx[c][:, 2 * h + jj, :])
+                for u in range(2):
+                    nc.tensor.transpose(xtb[c, h][:, jj, u, :], w[:, u : H // 2 : 2], ident[:])
+
+        def a2s(c, h):
+            if c not in xg:
+                xg[c] = work.tile([P, 4 * P, T], BF16, name="xg", align_bytes=64, bufs=3)
+            n = min(2, SIZES[c] - 2 * h)
+            dst = words(xg[c][:, h * 256 : h * 256 + n * P, :]).rearrange("p (j r) u -> p j r u", j=n)
+            nc.scalar.copy(out=dst, in_=xtb[c, h][:, :n].rearrange("p j u r -> p j r u"))
+
+        def a3(c):
+            n = SIZES[c] * P
+            xc[c] = work.tile([P, 4 * P], U32, name="xc", align_bytes=64, bufs=4)
+            xs[c] = work.tile([P, 4 * P], U8, name="xs", align_bytes=64, bufs=4)
+            nc.vector.quantize_mx(out=xc[c][:, :n].bitcast(FP8X4), scales=xs[c][:, :n], in_=xg[c][:, :n, :].rearrange("p n t -> p (n t)"))
+
+        def bp(c, j):
+            s1b[c, j] = ps_s.tile([P, H], F32, name="s1")
+            nc.tensor.matmul_mx(
+                out=s1b[c, j][:],
+                lhsT=xc[c][:, j * P : (j + 1) * P].bitcast(FP8X4),
+                lhsT_scale=xs[c][:, j * P : (j + 1) * P],
+                rhs=w_codes[:].bitcast(FP8X4),
+                rhs_scale=w_scales[:],
+                start=True,
+                stop=True,
+            )
+
+        def bv(c, j):
+            hb[c, j] = work.tile([P, H], F32, name="hb", bufs=4)
+            nc.vector.tensor_tensor(out=hb[c, j][:], in0=s1b[c, j][:], in1=bias[:], op=ALU.add)
+
+        def bs(c, j):
+            if c not in hh:
+                hh[c] = work.tile([P, 4, H], F32, name="hh", bufs=3)
+                sm[c] = stat.tile([P, 4], F32, name="sm")
+                nm[c] = stat.tile([P, 4], F32, name="nm")
+                sq[c] = stat.tile([P, 4], F32, name="sq")
+                rs[c] = stat.tile([P, 4], F32, name="rs")
+            nc.scalar.activation(out=hh[c][:, j, :], in_=hb[c, j][:], func=ACT.Tanh, accum_out=sm[c][:, j : j + 1])
+
+        def cgN(c):
+            n = SIZES[c]
+            nc.gpsimd.tensor_scalar(out=nm[c][:, :n], in0=sm[c][:, :n], scalar1=-1.0 / H, scalar2=0.0, op0=ALU.mult, op1=ALU.add)
+
+        def cq(c, j):
+            junk = work.tile([P, H], BF16, name="junk", bufs=2)
+            nc.scalar.activation(out=junk[:], in_=hh[c][:, j, :], func=ACT.Square, scale=-float(H), bias=sm[c][:, j : j + 1], accum_out=sq[c][:, j : j + 1])
+
+        def cgA(c):
+            n = SIZES[c]
+            nc.gpsimd.tensor_scalar(out=rs[c][:, :n], in0=sq[c][:, :n], scalar1=1.0 / H**3, scalar2=EPS, op0=ALU.mult, op1=ALU.add)
+
+        def cgP(c):
+            n = SIZES[c]
+            nc.gpsimd.tensor_tensor(out=rs[c][:, :n], in0=rs[c][:, :n], in1=half[:, :n], op=ALU.pow)
+
+        def cs(c, j):
+            if c not in zz:
+                zz[c] = work.tile([P, 4, H], F32, name="zz", bufs=3)
+            eng = nc.gpsimd if "GVGV"[j] == "G" else nc.vector
+            eng.tensor_scalar(
+                out=zz[c][:, j, :], in0=hh[c][:, j, :], scalar1=nm[c][:, j : j + 1], scalar2=rs[c][:, j : j + 1], op0=ALU.add, op1=ALU.mult
+            )
+
+        def dp(c, t):
+            fmb[c, t] = ps_f.tile([P, 4 * P], F32, name="fm")
+            for j in range(SIZES[c]):
+                nc.tensor.transpose(fmb[c, t][:, j * P : (j + 1) * P], zz[c][:, j, t * P : (t + 1) * P], ident[:])
+
+        affine_on_vector = {"even": [], "odd": [(3, 1)], "last": []}
+
+        def ds(c, t, o):
+            n = SIZES[c] * P
+            if (c, o) not in yy:
+                yy[c, o] = work.tile([P, T, 4 * P], BF16, name="yy%d" % o, bufs=3)
+            dst, src = yy[c, o][:, t, :n], fmb[c, t][:, :n]
+            scl, sft = g_col[:, o, t : t + 1], b_col[:, o, t : t + 1]
+            if (t, o) in affine_on_vector["last" if c == nch - 1 else ("odd" if c % 2 else "even")]:
+                nc.vector.tensor_scalar(out=dst, in0=src, scalar1=scl, scalar2=sft, op0=ALU.mult, op1=ALU.add)
+            else:
+                nc.scalar.activation(out=dst, in_=src, func=ACT.Identity, scale=scl, bias=sft)
+
+        parts = [[4],[4]]
+
+        def e1(c, o, part):
+            if (c, o) not in yg:
+                yg[c, o] = work.tile([P, 4 * P, T], BF16, name="yg%d" % o, align_bytes=64, bufs=3)
+            a = sum(parts[o][:part]) * 32 * SIZES[c]
+            ns = slice(a, a + parts[o][part] * 32 * SIZES[c])
+            nc.vector.tensor_copy(
+                out=yg[c, o][:, ns, :].rearrange("p (n i) t -> p n t i", i=4),
+                in_=yy[c, o][:, :, ns].rearrange("p t (n i) -> p n t i", i=4),
+            )
+
+        def e2(c, o):
+            n = SIZES[c] * P
+            yc[c, o] = work.tile([P, 4 * P], U32, name="yc%d" % o, align_bytes=64, bufs=3)
+            ys[c, o] = work.tile([P, 4 * P], U8, name="ys%d" % o, align_bytes=64, bufs=3)
+            nc.vector.quantize_mx(out=yc[c, o][:, :n].bitcast(FP8X4), scales=ys[c, o][:, :n], in_=yg[c, o][:, :n, :].rearrange("p n t -> p (n t)"))
+
+        def fp(c):
+            xo = ps_a.tile([P, 2, 2, P], F32, name="xt")
+            ob[c] = xo[:].rearrange("p a b r -> p (a b) r")
+            for j in range(SIZES[c]):
+                for o in range(2):
+                    nc.tensor.matmul_mx(
+                        out=ob[c][:, j, :],
+                        lhsT=yc[c, o][:, j * P : (j + 1) * P].bitcast(FP8X4),
+                        lhsT_scale=ys[c, o][:, j * P : (j + 1) * P],
+                        rhs=f_codes[:, o * P : (o + 1) * P].bitcast(FP8X4),
+                        rhs_scale=f_scales[:, o * P : (o + 1) * P],
+                        start=(o == 0),
+                        stop=(o == 1),
+                    )
+
+        def fv(c):
+            n = SIZES[c]
+            osb[c] = work.tile([P, 4, D_OUT], F32, name="osb", bufs=3)
+            nc.vector.tensor_tensor(out=osb[c][:, :n, :], in0=ob[c][:, :n, :], in1=fcb[:, :n, :], op=ALU.add)
+
+        def st_out(c):
+            nc.sync.dma_start(out=rows(out, c), in_=osb[c][:, : SIZES[c], :])
+
+        def turn_weights(src, pieces, grp):
+            xt = ps_f.tile([P, 4 * P], F32, name="fm")
+            v = xt[:].rearrange("p (a u r) -> p a u r", a=2, u=2)
+            for a in range(2):
+                for u in range(2):
+                    nc.tensor.transpose(v[:, a, u, :], pieces[a][:, u : H // 2 : 2], ident[:])
+            nc.scalar.copy(out=words(grp).rearrange("p (j r) u -> p j r u", j=2), in_=v.rearrange("p j u r -> p j r u"))
+
+        def weights():
+            for h in range(2):
+                turn_weights(None, [words(w_sb[:, 2 * h + a, :]) for a in range(2)], w_grp[:, h * 256 : h * 256 + 256, :])
+        def weights_quantised():
+            nc.vector.quantize_mx(out=w_codes[:].bitcast(FP8X4), scales=w_scales[:], in_=w_grp[:].rearrange("p n t -> p (n t)"))
+
+        def small_constants():
+            bk = ps_f.tile([P, 4 * P], F32, name="fm")
+            nc.tensor.matmul(bk[:], lhsT=ones[:], rhs=row_b[:], start=True, stop=True)
+            nc.scalar.copy(out=bias[:].rearrange("p (t m) -> p t m", t=T), in_=bk[:].rearrange("p (m t) -> p t m", t=T))
+
+        def late_constants():
+            nc.gpsimd.tensor_copy(out=g_col[:], in_=g_raw[:])
+            nc.gpsimd.tensor_copy(out=b_col[:], in_=b_raw[:])
+            fk = ps_f.tile([P, 4 * P], F32, name="fm")
+            for j in range(4):
+                nc.tensor.matmul(fk[:, j * P : (j + 1) * P], lhsT=ones[:], rhs=row_f[:], start=True, stop=True)
+            nc.scalar.copy(out=fcb[:].rearrange("p j f -> p (j f)"), in_=fk[:])
+            fw = words(f_sb[:])
+            turn_weights(None, [fw[:, 256 * o : 256 * (o + 1)] for o in range(2)], f_grp[:])
+            nc.vector.quantize_mx(out=f_codes[:].bitcast(FP8X4), scales=f_scales[:], in_=f_grp[:].rearrange("p n t -> p (n t)"))
+
+        steps = [
+            (e2, (0,), 6),
+            (dp, (3,), 5),
+            (cgP, (), 4),
+            (a2p, (1,), 1),
+            (load, (), 0),
+            (bp, (2,), 3),
+            (ds, (2, 1), 5),
+            (a2s, (0,), 1),
+            (ds, (1, 1), 5),
+            (ds, (2, 0), 5),
+            (bv, (3,), 3),
+            (cs, (2,), 4),
+            (ds, (3, 1), 5),
+            (ds, (1, 0), 5),
+            (bv, (2,), 3),
+            (bp, (0,), 2),
+            (bs, (0,), 3),
+            (ds, (3, 0), 5),
+            (a2s, (1,), 1),
+            (bs, (1,), 3),
+            (cs, (1,), 4),
+            (a1, (0,), 0),
+            (bp, (3,), 2),
+            (cq, (0,), 3),
+            (cs, (3,), 4),
+            (bs, (3,), 3),
+            (cq, (1,), 3),
+            (cs, (0,), 4),
+            (e1, (1, 0), 5),
+            (e1, (0, 0), 5),
+            (a1, (1,), 0),
+            (dp, (0,), 4),
+            (fp, (), 6),
+            (bs, (2,), 3),
+            (dp, (2,), 4),
+            (a2p, (0,), 0),
+            (e2, (1,), 5),
+            (bv, (0,), 2),
+            (cq, (3,), 3),
+            (cq, (2,), 3),
+            (ds, (0, 1), 4),
+            (a3, (), 1),
+            (bp, (1,), 2),
+            (fv, (), 6),
+            (bv, (1,), 2),
+            (ds, (0, 0), 4),
+            (st_out, (), 6),
+            (dp, (1,), 4),
+            (cgN, (), 3),
+            (cgA, (), 3),
+        ]
+        ctx.enter_context(tc.manual_schedule())
+        a1(0, 0)
+        a2p(0, 0)
+        a2s(0, 0)
+        a1(1, 0)
+        a3(0)
+        weights()
+        weights_quantised()
+        small_constants()
+        early = [(a1, 0, 0), (a2p, 0, 0), (a2s, 0, 0), (a3, 0), (a1, 1, 0)]
+        for i in range(nch + 7):
+            for fn, args, lag in steps:
+                c = i - lag
+                if not 0 <= c < nch or (fn, c, *args) in early or (fn is load and c <= 1):
+                    continue
+                if fn in (a1, a2p, a2s) and 2 * args[0] >= SIZES[c] or fn in (bp, bv, bs, cq, cs) and args[0] >= SIZES[c]:
+                    continue
+                fn(c, *args)
+            if i == 1:
+                late_constants()

@@ -32,20 +32,21 @@ def tile_rnnclassifier_pa_t_kernel(tc, h1_bytes, h1_scale, W_ih1, b_ih1, b_hh1, 
     with ExitStack() as ctx:
         const = ctx.enter_context(tc.tile_pool(name="const", bufs=1))
         work = ctx.enter_context(tc.tile_pool(name="work", bufs=2))
-        stat = ctx.enter_context(tc.tile_pool(name="stat", bufs=4))
-        ps_a = ctx.enter_context(tc.psum_pool(name="ps_a", bufs=2))
-        ps_s = ctx.enter_context(tc.psum_pool(name="ps_s", bufs=3))
+        stat = ctx.enter_context(tc.tile_pool(name="stat", bufs=3))
+        ps_x = ctx.enter_context(tc.psum_pool(name="ps_x", bufs=2))
+        ps_s = ctx.enter_context(tc.psum_pool(name="ps_s", bufs=2))
         ps_f = ctx.enter_context(tc.psum_pool(name="ps_f", bufs=3))
+        ps_o = ctx.enter_context(tc.psum_pool(name="ps_o", bufs=1))
+        ctx.enter_context(tc.manual_schedule())
 
         xb, hx, xg, xc, xs = {}, {}, {}, {}, {}
-        hb, hh, zz, sm, nm, sq, rs, nb = {}, {}, {}, {}, {}, {}, {}, {}
-        mv = {}
+        hb, hh, zz, sm, nm, sq, rs = {}, {}, {}, {}, {}, {}, {}
         yy, yg, yc, ys = {}, {}, {}, {}
         osb, fmb, xtb, s1b, ob = {}, {}, {}, {}, {}
 
         def load(c):
-            xb[c] = work.tile([P, 4, H], U8, name="x_bytes", align_bytes=64, bufs=6)
-            nc.sync.dma_start(out=xb[c][:, : SIZES[c], :], in_=rows(h1_bytes, c))
+            xb[c] = work.tile([P, SIZES[c] * H], U8, name="x_bytes", align_bytes=64, bufs=4)
+            nc.sync.dma_start(out=xb[c][:].rearrange("p (j k) -> p j k", k=H), in_=rows(h1_bytes, c))
 
         row_b = const.tile([P, H], BF16)
         nc.vector.memset(row_b[:], 0.0)
@@ -57,12 +58,10 @@ def tile_rnnclassifier_pa_t_kernel(tc, h1_bytes, h1_scale, W_ih1, b_ih1, b_hh1, 
         make_identity(nc, ident[:])
         half = const.tile([P, 4], F32)
         nc.gpsimd.memset(half[:], -0.5)
-        dummy = const.tile([P, 1], F32)
-        nc.gpsimd.memset(dummy[:], 0.0)
 
         load(0)
-        scale = const.tile([P, 2, H], F32)
-        nc.sync.dma_start(out=scale[:, 0, :], in_=h1_scale.rearrange("o k -> (o k)").partition_broadcast(P))
+        s4 = const.tile([P, T], F32)
+        nc.sync.dma_start(out=s4[:], in_=h1_scale.rearrange("o (p t) -> p (o t)", t=T))
         w_sb = const.tile([P, T, H], BF16)
         nc.sync.dma_start(out=w_sb[:], in_=W_ih1.rearrange("(m t) k -> m t k", t=T))
         nc.scalar.dma_start(out=row_b[0:1, :], in_=b_ih1.rearrange("(o k) -> o k", o=1))
@@ -71,12 +70,12 @@ def tile_rnnclassifier_pa_t_kernel(tc, h1_bytes, h1_scale, W_ih1, b_ih1, b_hh1, 
         f_sb = const.tile([P, H2], BF16)
         nc.sync.dma_start(out=f_sb[:], in_=fc_W)
         g_raw = const.tile([P, 2, T], BF16)
-        nc.gpsimd.dma_start(out=g_raw[:], in_=ln_g.rearrange("(o p t) -> p o t", o=2, t=T))
+        nc.sync.dma_start(out=g_raw[:], in_=ln_g.rearrange("(o p t) -> p o t", o=2, t=T))
         b_raw = const.tile([P, 2, T], BF16)
-        nc.gpsimd.dma_start(out=b_raw[:], in_=ln_b.rearrange("(o p t) -> p o t", o=2, t=T))
-        nc.gpsimd.dma_start(out=row_f[0:1, :], in_=fc_b.rearrange("(o k) -> o k", o=1))
-        nc.scalar.activation(out=dummy[:], in_=dummy[:], func=ACT.Tanh)
-        nc.scalar.copy(out=scale[:, 1, :], in_=scale[:, 0, :])
+        nc.sync.dma_start(out=b_raw[:], in_=ln_b.rearrange("(o p t) -> p o t", o=2, t=T))
+        nc.sync.dma_start(out=row_f[0:1, :], in_=fc_b.rearrange("(o k) -> o k", o=1))
+        scale = const.tile([P, 2 * P, T], F32)
+        nc.scalar.copy(out=scale[:], in_=s4[:].unsqueeze(1).to_broadcast([P, 2 * P, T]))
         bias = const.tile([P, H], F32)
         g_col = const.tile([P, 2, T], F32)
         b_col = const.tile([P, 2, T], F32)
@@ -92,40 +91,35 @@ def tile_rnnclassifier_pa_t_kernel(tc, h1_bytes, h1_scale, W_ih1, b_ih1, b_hh1, 
         def words(ap):
             return ap.bitcast(F32)
 
-        def a1(c, h):
-            if c not in hx:
-                hx[c] = work.tile([P, 4, H], BF16, name="hx", align_bytes=64, bufs=3)
-            n = min(2, SIZES[c] - 2 * h)
-            dst = hx[c][:, 2 * h : 2 * h + n, :].rearrange("p j k -> p (j k)")
-            code = xb[c][:, 2 * h : 2 * h + n, :].rearrange("p j k -> p (j k)").bitcast(FP8)
-            if c == 0:
-                for j in range(2 * h, 2 * h + n):
-                    nc.vector.tensor_tensor(out=hx[c][:, j, :], in0=xb[c][:, j, :].bitcast(FP8), in1=scale[:, 0, :], op=ALU.mult)
-                return
-            nc.vector.tensor_tensor(out=dst, in0=code, in1=scale[:, :n, :].rearrange("p a k -> p (a k)"), op=ALU.mult)
+        def cast(c):
+            hx[c] = work.tile([P, SIZES[c] * H], BF16, name="hx", align_bytes=64)
+            nc.vector.tensor_copy(out=hx[c][:], in_=xb[c][:].bitcast(FP8))
 
-        def a2p(c, h):
-            n = min(2, SIZES[c] - 2 * h)
-            xtb[c, h] = ps_a.tile([P, 2, 2, P], F32, name="xt")
-            for jj in range(n):
-                w = words(hx[c][:, 2 * h + jj, :])
+        def turn_x(c, h):
+            xtb[c, h] = ps_x.tile([P, 2, 2 * P], F32, name="xt")
+            for jj in range(2):
+                j = 2 * h + jj
+                w = words(hx[c][:, j * H : (j + 1) * H])
                 for u in range(2):
-                    nc.tensor.transpose(xtb[c, h][:, jj, u, :], w[:, u : H // 2 : 2], ident[:])
+                    nc.tensor.transpose(xtb[c, h][:, u, jj * P : (jj + 1) * P], w[:, u : H // 2 : 2], ident[:])
 
-        def a2s(c, h):
+        def scale_out(c, h):
             if c not in xg:
-                xg[c] = work.tile([P, 4 * P, T], BF16, name="xg", align_bytes=64, bufs=3)
-            n = min(2, SIZES[c] - 2 * h)
-            dst = words(xg[c][:, h * 256 : h * 256 + n * P, :]).rearrange("p (j r) u -> p j r u", j=n)
-            nc.scalar.copy(out=dst, in_=xtb[c, h][:, :n].rearrange("p j u r -> p j r u"))
+                xg[c] = work.tile([P, SIZES[c] * P, T], BF16, name="xg", align_bytes=64)
+            nc.vector.tensor_tensor(
+                out=xg[c][:, h * 2 * P : (h + 1) * 2 * P, :].rearrange("p n (u e) -> p n u e", e=2),
+                in0=xtb[c, h][:].bitcast(BF16).rearrange("p u (n e) -> p n u e", e=2),
+                in1=scale[:].rearrange("p n (u e) -> p n u e", e=2),
+                op=ALU.mult,
+            )
 
-        def a3(c):
+        def quant_x(c):
             n = SIZES[c] * P
-            xc[c] = work.tile([P, 4 * P], U32, name="xc", align_bytes=64, bufs=4)
-            xs[c] = work.tile([P, 4 * P], U8, name="xs", align_bytes=64, bufs=4)
-            nc.vector.quantize_mx(out=xc[c][:, :n].bitcast(FP8X4), scales=xs[c][:, :n], in_=xg[c][:, :n, :].rearrange("p n t -> p (n t)"))
+            xc[c] = work.tile([P, n], U32, name="xc", align_bytes=64)
+            xs[c] = work.tile([P, n], U8, name="xs", align_bytes=64)
+            nc.vector.quantize_mx(out=xc[c][:].bitcast(FP8X4), scales=xs[c][:], in_=xg[c][:].rearrange("p n t -> p (n t)"))
 
-        def bp(c, j):
+        def mm1(c, j):
             s1b[c, j] = ps_s.tile([P, H], F32, name="s1")
             nc.tensor.matmul_mx(
                 out=s1b[c, j][:],
@@ -137,103 +131,98 @@ def tile_rnnclassifier_pa_t_kernel(tc, h1_bytes, h1_scale, W_ih1, b_ih1, b_hh1, 
                 stop=True,
             )
 
-        def bv(c, j):
+        def add_bias(c, j):
             hb[c, j] = work.tile([P, H], F32, name="hb", bufs=4)
             nc.vector.tensor_tensor(out=hb[c, j][:], in0=s1b[c, j][:], in1=bias[:], op=ALU.add)
 
-        def bs(c, j):
-            if c not in hh:
-                hh[c] = work.tile([P, 4, H], F32, name="hh", bufs=3)
+        def tanh(c, j):
+            if c not in sm:
                 sm[c] = stat.tile([P, 4], F32, name="sm")
-                nm[c] = stat.tile([P, 4], F32, name="nm")
                 sq[c] = stat.tile([P, 4], F32, name="sq")
-                rs[c] = stat.tile([P, 4], F32, name="rs")
-            nc.scalar.activation(out=hh[c][:, j, :], in_=hb[c, j][:], func=ACT.Tanh, accum_out=sm[c][:, j : j + 1])
+            hh[c, j] = work.tile([P, H], F32, name="hh", bufs=8)
+            nc.scalar.activation(out=hh[c, j][:], in_=hb[c, j][:], func=ACT.Tanh, accum_out=sm[c][:, j : j + 1])
 
-        def cgN(c):
+        def square(c, j):
+            junk = work.tile([P, H], BF16, name="junk")
+            nc.scalar.activation(out=junk[:], in_=hh[c, j][:], func=ACT.Square, scale=-float(H), bias=sm[c][:, j : j + 1], accum_out=sq[c][:, j : j + 1])
+
+        def moments(c):
             n = SIZES[c]
-            nc.gpsimd.tensor_scalar(out=nm[c][:, :n], in0=sm[c][:, :n], scalar1=-1.0 / H, scalar2=0.0, op0=ALU.mult, op1=ALU.add)
+            nm[c] = stat.tile([P, 4], F32, name="nm")
+            rs[c] = stat.tile([P, 4], F32, name="rs")
+            nc.scalar.activation(out=rs[c][:, :n], in_=sq[c][:, :n], func=ACT.Copy, scale=1.0 / H**3, bias=EPS)
+            nc.scalar.activation(out=nm[c][:, :n], in_=sm[c][:, :n], func=ACT.Copy, scale=-1.0 / H)
 
-        def cq(c, j):
-            junk = work.tile([P, H], BF16, name="junk", bufs=2)
-            nc.scalar.activation(out=junk[:], in_=hh[c][:, j, :], func=ACT.Square, scale=-float(H), bias=sm[c][:, j : j + 1], accum_out=sq[c][:, j : j + 1])
-
-        def cgA(c):
-            n = SIZES[c]
-            nc.gpsimd.tensor_scalar(out=rs[c][:, :n], in0=sq[c][:, :n], scalar1=1.0 / H**3, scalar2=EPS, op0=ALU.mult, op1=ALU.add)
-
-        def cgP(c):
+        def inv_root(c):
             n = SIZES[c]
             nc.gpsimd.tensor_tensor(out=rs[c][:, :n], in0=rs[c][:, :n], in1=half[:, :n], op=ALU.pow)
 
-        def cs(c, j):
-            if c not in zz:
-                zz[c] = work.tile([P, 4, H], F32, name="zz", bufs=3)
-            eng = nc.gpsimd if "GVGV"[j] == "G" else nc.vector
-            eng.tensor_scalar(
-                out=zz[c][:, j, :], in0=hh[c][:, j, :], scalar1=nm[c][:, j : j + 1], scalar2=rs[c][:, j : j + 1], op0=ALU.add, op1=ALU.mult
+        def normalise(c, j):
+            zz[c, j] = work.tile([P, H], F32, name="zz", bufs=8)
+            nc.vector.tensor_scalar(
+                out=zz[c, j][:], in0=hh[c, j][:], scalar1=nm[c][:, j : j + 1], scalar2=rs[c][:, j : j + 1], op0=ALU.add, op1=ALU.mult
             )
 
-        def dp(c, t):
-            fmb[c, t] = ps_f.tile([P, 4 * P], F32, name="fm")
+        def turn_z(c, t):
+            fmb[c, t] = ps_f.tile([P, SIZES[c] * P], F32, name="fm")
             for j in range(SIZES[c]):
-                nc.tensor.transpose(fmb[c, t][:, j * P : (j + 1) * P], zz[c][:, j, t * P : (t + 1) * P], ident[:])
+                nc.tensor.transpose(fmb[c, t][:, j * P : (j + 1) * P], zz[c, j][:, t * P : (t + 1) * P], ident[:])
 
-        affine_on_vector = {"even": [], "odd": [(3, 1)], "last": []}
+        def affine(c, t):
+            if c not in yy:
+                yy[c] = work.tile([P, 2, T, SIZES[c] * P], BF16, name="yy")
+            for o in range(2):
+                nc.scalar.activation(out=yy[c][:, o, t, :], in_=fmb[c, t][:], func=ACT.Identity, scale=g_col[:, o, t : t + 1], bias=b_col[:, o, t : t + 1])
 
-        def ds(c, t, o):
+        def pool_share(c):
+            return SIZES[c] * P * 3 // 4 if c + 3 < nch - 1 else 0
+
+        def weave_pool(c):
             n = SIZES[c] * P
-            if (c, o) not in yy:
-                yy[c, o] = work.tile([P, T, 4 * P], BF16, name="yy%d" % o, bufs=3)
-            dst, src = yy[c, o][:, t, :n], fmb[c, t][:, :n]
-            scl, sft = g_col[:, o, t : t + 1], b_col[:, o, t : t + 1]
-            if (t, o) in affine_on_vector["last" if c == nch - 1 else ("odd" if c % 2 else "even")]:
-                nc.vector.tensor_scalar(out=dst, in0=src, scalar1=scl, scalar2=sft, op0=ALU.mult, op1=ALU.add)
-            else:
-                nc.scalar.activation(out=dst, in_=src, func=ACT.Identity, scale=scl, bias=sft)
-
-        parts = [[4],[4]]
-
-        def e1(c, o, part):
-            if (c, o) not in yg:
-                yg[c, o] = work.tile([P, 4 * P, T], BF16, name="yg%d" % o, align_bytes=64, bufs=3)
-            a = sum(parts[o][:part]) * 32 * SIZES[c]
-            ns = slice(a, a + parts[o][part] * 32 * SIZES[c])
-            nc.vector.tensor_copy(
-                out=yg[c, o][:, ns, :].rearrange("p (n i) t -> p n t i", i=4),
-                in_=yy[c, o][:, :, ns].rearrange("p t (n i) -> p n t i", i=4),
+            yg[c] = work.tile([P, 2, n, T], BF16, name="yg", align_bytes=64, bufs=1)
+            m = pool_share(c)
+            if m == 0:
+                return
+            nc.gpsimd.tensor_scalar(
+                out=yg[c][:, :, :m, :], in0=yy[c][:, :, :, :m].rearrange("p o t n -> p o n t"), scalar1=1.0, scalar2=0.0, op0=ALU.mult, op1=ALU.add
             )
 
-        def e2(c, o):
-            n = SIZES[c] * P
-            yc[c, o] = work.tile([P, 4 * P], U32, name="yc%d" % o, align_bytes=64, bufs=3)
-            ys[c, o] = work.tile([P, 4 * P], U8, name="ys%d" % o, align_bytes=64, bufs=3)
-            nc.vector.quantize_mx(out=yc[c, o][:, :n].bitcast(FP8X4), scales=ys[c, o][:, :n], in_=yg[c, o][:, :n, :].rearrange("p n t -> p (n t)"))
+        def weave_vector(c):
+            m = pool_share(c)
+            nc.vector.tensor_copy(
+                out=yg[c][:, :, m:, :].rearrange("p o (n i) t -> p o n t i", i=4),
+                in_=yy[c][:, :, :, m:].rearrange("p o t (n i) -> p o n t i", i=4),
+            )
 
-        def fp(c):
-            xo = ps_a.tile([P, 2, 2, P], F32, name="xt")
-            ob[c] = xo[:].rearrange("p a b r -> p (a b) r")
+        def quant_y(c):
+            n = SIZES[c] * P
+            yc[c] = work.tile([P, 2 * n], U32, name="yc", align_bytes=64)
+            ys[c] = work.tile([P, 2 * n], U8, name="ys", align_bytes=64)
+            nc.vector.quantize_mx(out=yc[c][:].bitcast(FP8X4), scales=ys[c][:], in_=yg[c][:].rearrange("p o n t -> p (o n t)"))
+
+        def mm2(c):
+            n = SIZES[c] * P
+            ob[c] = ps_o.tile([P, SIZES[c], D_OUT], F32, name="ob")
             for j in range(SIZES[c]):
                 for o in range(2):
+                    cols = slice(o * n + j * P, o * n + (j + 1) * P)
                     nc.tensor.matmul_mx(
                         out=ob[c][:, j, :],
-                        lhsT=yc[c, o][:, j * P : (j + 1) * P].bitcast(FP8X4),
-                        lhsT_scale=ys[c, o][:, j * P : (j + 1) * P],
+                        lhsT=yc[c][:, cols].bitcast(FP8X4),
+                        lhsT_scale=ys[c][:, cols],
                         rhs=f_codes[:, o * P : (o + 1) * P].bitcast(FP8X4),
                         rhs_scale=f_scales[:, o * P : (o + 1) * P],
                         start=(o == 0),
                         stop=(o == 1),
                     )
 
-        def fv(c):
+        def finish(c):
             n = SIZES[c]
-            osb[c] = work.tile([P, 4, D_OUT], F32, name="osb", bufs=3)
-            nc.vector.tensor_tensor(out=osb[c][:, :n, :], in0=ob[c][:, :n, :], in1=fcb[:, :n, :], op=ALU.add)
+            osb[c] = work.tile([P, n, D_OUT], F32, name="osb")
+            nc.vector.tensor_tensor(out=osb[c][:], in0=ob[c][:], in1=fcb[:, :n, :], op=ALU.add)
+            nc.sync.dma_start(out=rows(out, c), in_=osb[c][:])
 
-        def st_out(c):
-            nc.sync.dma_start(out=rows(out, c), in_=osb[c][:, : SIZES[c], :])
-
-        def turn_weights(src, pieces, grp):
+        def turn_weights(pieces, grp):
             xt = ps_f.tile([P, 4 * P], F32, name="fm")
             v = xt[:].rearrange("p (a u r) -> p a u r", a=2, u=2)
             for a in range(2):
@@ -241,16 +230,15 @@ def tile_rnnclassifier_pa_t_kernel(tc, h1_bytes, h1_scale, W_ih1, b_ih1, b_hh1, 
                     nc.tensor.transpose(v[:, a, u, :], pieces[a][:, u : H // 2 : 2], ident[:])
             nc.scalar.copy(out=words(grp).rearrange("p (j r) u -> p j r u", j=2), in_=v.rearrange("p j u r -> p j r u"))
 
-        def weights():
+        def first_weights():
             for h in range(2):
-                turn_weights(None, [words(w_sb[:, 2 * h + a, :]) for a in range(2)], w_grp[:, h * 256 : h * 256 + 256, :])
-        def weights_quantised():
-            nc.vector.quantize_mx(out=w_codes[:].bitcast(FP8X4), scales=w_scales[:], in_=w_grp[:].rearrange("p n t -> p (n t)"))
-
-        def small_constants():
+                turn_weights([words(w_sb[:, 2 * h + a, :]) for a in range(2)], w_grp[:, h * 256 : h * 256 + 256, :])
             bk = ps_f.tile([P, 4 * P], F32, name="fm")
             nc.tensor.matmul(bk[:], lhsT=ones[:], rhs=row_b[:], start=True, stop=True)
             nc.scalar.copy(out=bias[:].rearrange("p (t m) -> p t m", t=T), in_=bk[:].rearrange("p (m t) -> p t m", t=T))
+
+        def first_weights_quantised():
+            nc.vector.quantize_mx(out=w_codes[:].bitcast(FP8X4), scales=w_scales[:], in_=w_grp[:].rearrange("p n t -> p (n t)"))
 
         def late_constants():
             nc.gpsimd.tensor_copy(out=g_col[:], in_=g_raw[:])
@@ -260,78 +248,65 @@ def tile_rnnclassifier_pa_t_kernel(tc, h1_bytes, h1_scale, W_ih1, b_ih1, b_hh1, 
                 nc.tensor.matmul(fk[:, j * P : (j + 1) * P], lhsT=ones[:], rhs=row_f[:], start=True, stop=True)
             nc.scalar.copy(out=fcb[:].rearrange("p j f -> p (j f)"), in_=fk[:])
             fw = words(f_sb[:])
-            turn_weights(None, [fw[:, 256 * o : 256 * (o + 1)] for o in range(2)], f_grp[:])
+            turn_weights([fw[:, 256 * o : 256 * (o + 1)] for o in range(2)], f_grp[:])
+
+        def late_weights_quantised():
             nc.vector.quantize_mx(out=f_codes[:].bitcast(FP8X4), scales=f_scales[:], in_=f_grp[:].rearrange("p n t -> p (n t)"))
 
-        steps = [
-            (e2, (0,), 6),
-            (dp, (3,), 5),
-            (cgP, (), 4),
-            (a2p, (1,), 1),
-            (load, (), 0),
-            (bp, (2,), 3),
-            (ds, (2, 1), 5),
-            (a2s, (0,), 1),
-            (ds, (1, 1), 5),
-            (ds, (2, 0), 5),
-            (bv, (3,), 3),
-            (cs, (2,), 4),
-            (ds, (3, 1), 5),
-            (ds, (1, 0), 5),
-            (bv, (2,), 3),
-            (bp, (0,), 2),
-            (bs, (0,), 3),
-            (ds, (3, 0), 5),
-            (a2s, (1,), 1),
-            (bs, (1,), 3),
-            (cs, (1,), 4),
-            (a1, (0,), 0),
-            (bp, (3,), 2),
-            (cq, (0,), 3),
-            (cs, (3,), 4),
-            (bs, (3,), 3),
-            (cq, (1,), 3),
-            (cs, (0,), 4),
-            (e1, (1, 0), 5),
-            (e1, (0, 0), 5),
-            (a1, (1,), 0),
-            (dp, (0,), 4),
-            (fp, (), 6),
-            (bs, (2,), 3),
-            (dp, (2,), 4),
-            (a2p, (0,), 0),
-            (e2, (1,), 5),
-            (bv, (0,), 2),
-            (cq, (3,), 3),
-            (cq, (2,), 3),
-            (ds, (0, 1), 4),
-            (a3, (), 1),
-            (bp, (1,), 2),
-            (fv, (), 6),
-            (bv, (1,), 2),
-            (ds, (0, 0), 4),
-            (st_out, (), 6),
-            (dp, (1,), 4),
-            (cgN, (), 3),
-            (cgA, (), 3),
-        ]
-        ctx.enter_context(tc.manual_schedule())
-        a1(0, 0)
-        a2p(0, 0)
-        a2s(0, 0)
-        a1(1, 0)
-        a3(0)
-        weights()
-        weights_quantised()
-        small_constants()
-        early = [(a1, 0, 0), (a2p, 0, 0), (a2s, 0, 0), (a3, 0), (a1, 1, 0)]
-        for i in range(nch + 7):
-            for fn, args, lag in steps:
-                c = i - lag
-                if not 0 <= c < nch or (fn, c, *args) in early or (fn is load and c <= 1):
-                    continue
-                if fn in (a1, a2p, a2s) and 2 * args[0] >= SIZES[c] or fn in (bp, bv, bs, cq, cs) and args[0] >= SIZES[c]:
-                    continue
+        def on(fn, c, *args):
+            if 0 <= c < nch:
                 fn(c, *args)
+
+        def on_tile(fn, c, j):
+            if 0 <= c < nch and j < SIZES[c]:
+                fn(c, j)
+
+        def on_pair(fn, c, h):
+            if 0 <= c < nch and 2 * h < SIZES[c]:
+                fn(c, h)
+
+        cast(0)
+        first_weights()
+        for i in range(nch + 6):
+            c_cast, c_turn, c_quant, c_tanh, c_norm, c_affine, c_weave, c_out = range(i + 1, i - 7, -1)
+            on(load, i + 2)
+            on(weave_pool, c_weave)
+            on(mm2, c_out)
+            on_pair(scale_out, c_quant, 0)
+            on(affine, c_affine, 0)
+            on(moments, c_norm)
+            on(inv_root, c_norm)
+            on_tile(add_bias, c_tanh, 0)
+            on_tile(mm1, c_tanh, 2)
+            on_pair(scale_out, c_quant, 1)
+            on(affine, c_affine, 1)
+            on_tile(add_bias, c_tanh, 1)
+            on_tile(mm1, c_tanh, 3)
+            on(turn_z, c_affine, 3)
+            on_pair(turn_x, c_turn, 0)
+            on_pair(turn_x, c_turn, 1)
+            on(affine, c_affine, 2)
+            on(finish, c_out)
+            on_tile(add_bias, c_tanh, 2)
+            on_tile(add_bias, c_tanh, 3)
+            for j in range(4):
+                on_tile(tanh, c_tanh, j)
+            on(quant_x, c_quant)
+            if i == 1:
+                first_weights_quantised()
+            for j in range(4):
+                on_tile(normalise, c_norm, j)
+            on(weave_vector, c_weave)
+            on(cast, c_cast)
+            on(quant_y, c_weave)
+            on(affine, c_affine, 3)
+            for j in range(4):
+                on_tile(square, c_tanh, j)
+            for t in range(3):
+                on(turn_z, c_norm, t)
+            on_tile(mm1, c_quant, 0)
+            on_tile(mm1, c_quant, 1)
             if i == 1:
                 late_constants()
+            if i == 2:
+                late_weights_quantised()

@@ -9,6 +9,7 @@ T = 4
 EPS = 1e-5
 FLOPS = 2 * B * H * H + 2 * B * H2 * D_OUT
 SIZES = [2] + [4] * 15 + [2]
+CAST_ON_SCALAR = (2, 3)
 
 F32 = mybir.dt.float32
 BF16 = mybir.dt.bfloat16
@@ -59,14 +60,21 @@ def tile_rnnclassifier_pa_t_kernel(tc, h1_bytes, h1_scale, W_ih1, b_ih1, b_hh1, 
         half = const.tile([P, 4], F32)
         nc.gpsimd.memset(half[:], -0.5)
 
+        w_sb = {}
+
+        def load_w(h):
+            w_sb[h] = const.tile([P, 2, H], BF16, name="w_sb%d" % h)
+            nc.sync.dma_start(out=w_sb[h][:], in_=W_ih1.rearrange("(m t) k -> m t k", t=T)[:, 2 * h : 2 * h + 2, :])
+
+        load_w(0)
         load(0)
         s4 = const.tile([P, T], F32)
         nc.sync.dma_start(out=s4[:], in_=h1_scale.rearrange("o (p t) -> p (o t)", t=T))
-        w_sb = const.tile([P, T, H], BF16)
-        nc.sync.dma_start(out=w_sb[:], in_=W_ih1.rearrange("(m t) k -> m t k", t=T))
+        load_w(1)
         nc.scalar.dma_start(out=row_b[0:1, :], in_=b_ih1.rearrange("(o k) -> o k", o=1))
         nc.scalar.dma_start(out=row_b[1:2, :], in_=b_hh1.rearrange("(o k) -> o k", o=1))
         load(1)
+        load(2)
         f_sb = const.tile([P, H2], BF16)
         nc.sync.dma_start(out=f_sb[:], in_=fc_W)
         g_raw = const.tile([P, 2, T], BF16)
@@ -75,7 +83,6 @@ def tile_rnnclassifier_pa_t_kernel(tc, h1_bytes, h1_scale, W_ih1, b_ih1, b_hh1, 
         nc.sync.dma_start(out=b_raw[:], in_=ln_b.rearrange("(o p t) -> p o t", o=2, t=T))
         nc.sync.dma_start(out=row_f[0:1, :], in_=fc_b.rearrange("(o k) -> o k", o=1))
         scale = const.tile([P, 2 * P, T], F32)
-        nc.scalar.copy(out=scale[:], in_=s4[:].unsqueeze(1).to_broadcast([P, 2 * P, T]))
         bias = const.tile([P, H], F32)
         g_col = const.tile([P, 2, T], F32)
         b_col = const.tile([P, 2, T], F32)
@@ -93,11 +100,15 @@ def tile_rnnclassifier_pa_t_kernel(tc, h1_bytes, h1_scale, W_ih1, b_ih1, b_hh1, 
 
         def cast(c):
             hx[c] = work.tile([P, SIZES[c] * H], BF16, name="hx", align_bytes=64)
-            nc.vector.tensor_copy(out=hx[c][:], in_=xb[c][:].bitcast(FP8))
+            if c in CAST_ON_SCALAR:
+                nc.scalar.copy(out=hx[c][:], in_=xb[c][:].bitcast(FP8))
+            else:
+                nc.vector.tensor_copy(out=hx[c][:], in_=xb[c][:].bitcast(FP8))
 
         def turn_x(c, h):
-            xtb[c, h] = ps_x.tile([P, 2, 2 * P], F32, name="xt")
-            for jj in range(2):
+            m = min(2, SIZES[c] - 2 * h)
+            xtb[c, h] = ps_x.tile([P, 2, m * P], F32, name="xt")
+            for jj in range(m):
                 j = 2 * h + jj
                 w = words(hx[c][:, j * H : (j + 1) * H])
                 for u in range(2):
@@ -106,10 +117,11 @@ def tile_rnnclassifier_pa_t_kernel(tc, h1_bytes, h1_scale, W_ih1, b_ih1, b_hh1, 
         def scale_out(c, h):
             if c not in xg:
                 xg[c] = work.tile([P, SIZES[c] * P, T], BF16, name="xg", align_bytes=64)
+            n = min(2, SIZES[c] - 2 * h) * P
             nc.vector.tensor_tensor(
-                out=xg[c][:, h * 2 * P : (h + 1) * 2 * P, :].rearrange("p n (u e) -> p n u e", e=2),
+                out=xg[c][:, h * 2 * P : h * 2 * P + n, :].rearrange("p n (u e) -> p n u e", e=2),
                 in0=xtb[c, h][:].bitcast(BF16).rearrange("p u (n e) -> p n u e", e=2),
-                in1=scale[:].rearrange("p n (u e) -> p n u e", e=2),
+                in1=scale[:, :n, :].rearrange("p n (u e) -> p n u e", e=2),
                 op=ALU.mult,
             )
 
@@ -168,14 +180,23 @@ def tile_rnnclassifier_pa_t_kernel(tc, h1_bytes, h1_scale, W_ih1, b_ih1, b_hh1, 
             for j in range(SIZES[c]):
                 nc.tensor.transpose(fmb[c, t][:, j * P : (j + 1) * P], zz[c, j][:, t * P : (t + 1) * P], ident[:])
 
+        def on_vector(c, t):
+            return t == 3 and nch - 4 <= c < nch - 2
+
         def affine(c, t):
             if c not in yy:
-                yy[c] = work.tile([P, 2, T, SIZES[c] * P], BF16, name="yy")
+                yy[c] = work.tile([P, 2, T, SIZES[c] * P], BF16, name="yy", bufs=3)
             for o in range(2):
-                nc.scalar.activation(out=yy[c][:, o, t, :], in_=fmb[c, t][:], func=ACT.Identity, scale=g_col[:, o, t : t + 1], bias=b_col[:, o, t : t + 1])
+                gain, shift = g_col[:, o, t : t + 1], b_col[:, o, t : t + 1]
+                if on_vector(c, t):
+                    nc.vector.tensor_scalar(out=yy[c][:, o, t, :], in0=fmb[c, t][:], scalar1=gain, scalar2=shift, op0=ALU.mult, op1=ALU.add)
+                else:
+                    nc.scalar.activation(out=yy[c][:, o, t, :], in_=fmb[c, t][:], func=ACT.Identity, scale=gain, bias=shift)
 
         def pool_share(c):
-            return SIZES[c] * P * 3 // 4 if c + 3 < nch - 1 else 0
+            if c < nch - 5:
+                return SIZES[c] * P * 3 // 4
+            return SIZES[c] * P // 4 if c <= nch - 4 else 0
 
         def weave_pool(c):
             n = SIZES[c] * P
@@ -194,6 +215,11 @@ def tile_rnnclassifier_pa_t_kernel(tc, h1_bytes, h1_scale, W_ih1, b_ih1, b_hh1, 
                 in_=yy[c][:, :, :, m:].rearrange("p o t (n i) -> p o n t i", i=4),
             )
 
+        def weave_scalar(c):
+            yg[c] = work.tile([P, 2, SIZES[c] * P, T], BF16, name="yg_last", align_bytes=64, bufs=1)
+            for o in range(2):
+                nc.scalar.copy(out=yg[c][:, o].rearrange("p (n i) t -> p n t i", i=4), in_=yy[c][:, o].rearrange("p t (n i) -> p n t i", i=4))
+
         def quant_y(c):
             n = SIZES[c] * P
             yc[c] = work.tile([P, 2 * n], U32, name="yc", align_bytes=64)
@@ -202,7 +228,10 @@ def tile_rnnclassifier_pa_t_kernel(tc, h1_bytes, h1_scale, W_ih1, b_ih1, b_hh1, 
 
         def mm2(c):
             n = SIZES[c] * P
-            ob[c] = ps_o.tile([P, SIZES[c], D_OUT], F32, name="ob")
+            if c == nch - 1:
+                ob[c] = ps_x.tile([P, SIZES[c], D_OUT], F32, name="xt")
+            else:
+                ob[c] = ps_o.tile([P, SIZES[c], D_OUT], F32, name="ob")
             for j in range(SIZES[c]):
                 for o in range(2):
                     cols = slice(o * n + j * P, o * n + (j + 1) * P)
@@ -230,9 +259,10 @@ def tile_rnnclassifier_pa_t_kernel(tc, h1_bytes, h1_scale, W_ih1, b_ih1, b_hh1, 
                     nc.tensor.transpose(v[:, a, u, :], pieces[a][:, u : H // 2 : 2], ident[:])
             nc.scalar.copy(out=words(grp).rearrange("p (j r) u -> p j r u", j=2), in_=v.rearrange("p j u r -> p j r u"))
 
-        def first_weights():
-            for h in range(2):
-                turn_weights([words(w_sb[:, 2 * h + a, :]) for a in range(2)], w_grp[:, h * 256 : h * 256 + 256, :])
+        def first_weights(h):
+            turn_weights([words(w_sb[h][:, a, :]) for a in range(2)], w_grp[:, h * 256 : h * 256 + 256, :])
+
+        def first_bias():
             bk = ps_f.tile([P, 4 * P], F32, name="fm")
             nc.tensor.matmul(bk[:], lhsT=ones[:], rhs=row_b[:], start=True, stop=True)
             nc.scalar.copy(out=bias[:].rearrange("p (t m) -> p t m", t=T), in_=bk[:].rearrange("p (m t) -> p t m", t=T))
@@ -265,16 +295,20 @@ def tile_rnnclassifier_pa_t_kernel(tc, h1_bytes, h1_scale, W_ih1, b_ih1, b_hh1, 
             if 0 <= c < nch and 2 * h < SIZES[c]:
                 fn(c, h)
 
+        first_weights(0)
         cast(0)
-        first_weights()
-        for i in range(nch + 6):
+        nc.vector.tensor_copy(out=scale[:], in_=s4[:].unsqueeze(1).to_broadcast([P, 2 * P, T]))
+        turn_x(0, 0)
+        first_weights(1)
+        first_bias()
+        cast(1)
+        for i in range(1, nch + 1):
             c_cast, c_turn, c_quant, c_tanh, c_norm, c_affine, c_weave, c_out = range(i + 1, i - 7, -1)
             on(load, i + 2)
             on(weave_pool, c_weave)
             on(mm2, c_out)
             on_pair(scale_out, c_quant, 0)
             on(affine, c_affine, 0)
-            on(moments, c_norm)
             on(inv_root, c_norm)
             on_tile(add_bias, c_tanh, 0)
             on_tile(mm1, c_tanh, 2)
@@ -291,6 +325,8 @@ def tile_rnnclassifier_pa_t_kernel(tc, h1_bytes, h1_scale, W_ih1, b_ih1, b_hh1, 
             on_tile(add_bias, c_tanh, 3)
             for j in range(4):
                 on_tile(tanh, c_tanh, j)
+            if on_vector(c_affine, 3):
+                affine(c_affine, 3)
             on(quant_x, c_quant)
             if i == 1:
                 first_weights_quantised()
@@ -299,14 +335,59 @@ def tile_rnnclassifier_pa_t_kernel(tc, h1_bytes, h1_scale, W_ih1, b_ih1, b_hh1, 
             on(weave_vector, c_weave)
             on(cast, c_cast)
             on(quant_y, c_weave)
-            on(affine, c_affine, 3)
+            if not on_vector(c_affine, 3):
+                on(affine, c_affine, 3)
             for j in range(4):
                 on_tile(square, c_tanh, j)
+            on(moments, c_tanh)
             for t in range(3):
                 on(turn_z, c_norm, t)
             on_tile(mm1, c_quant, 0)
             on_tile(mm1, c_quant, 1)
-            if i == 1:
-                late_constants()
             if i == 2:
+                late_constants()
+            if i == 3:
                 late_weights_quantised()
+
+        last = nch - 1
+        weave_pool(last - 3)
+        mm2(last - 4)
+        affine(last - 2, 0)
+        inv_root(last - 1)
+        turn_z(last - 2, 3)
+        for j in range(SIZES[last]):
+            add_bias(last, j)
+        finish(last - 4)
+        for j in range(SIZES[last]):
+            tanh(last, j)
+        affine(last - 2, 3)
+        affine(last - 2, 1)
+        for j in range(SIZES[last]):
+            square(last, j)
+        affine(last - 2, 2)
+        moments(last)
+        inv_root(last)
+        for j in range(4):
+            normalise(last - 1, j)
+        weave_vector(last - 3)
+        for j in range(SIZES[last]):
+            normalise(last, j)
+        quant_y(last - 3)
+        for c in (last - 1, last):
+            for t in range(3):
+                turn_z(c, t)
+            affine(c, 0)
+            turn_z(c, 3)
+            mm2(c - 2)
+            for t in range(1, 4):
+                affine(c, t)
+            weave_pool(c - 1)
+            weave_vector(c - 1)
+            finish(c - 2)
+            quant_y(c - 1)
+        weave_scalar(last)
+        mm2(last - 1)
+        quant_y(last)
+        mm2(last)
+        finish(last - 1)
+        finish(last)

@@ -151,7 +151,7 @@ def tile_rnnclassifier_pa_t_kernel(tc, h1_bytes, h1_scale, W_ih1, b_ih1, b_hh1, 
             if c not in sm:
                 sm[c] = stat.tile([P, 4], F32, name="sm")
                 sq[c] = stat.tile([P, 4], F32, name="sq")
-            hh[c, j] = work.tile([P, H], F32, name="hh", bufs=8)
+            hh[c, j] = work.tile([P, H], F32, name="hh", bufs=12)
             nc.scalar.activation(out=hh[c, j][:], in_=hb[c, j][:], func=ACT.Tanh, accum_out=sm[c][:, j : j + 1])
 
         def square(c, j):
@@ -160,25 +160,40 @@ def tile_rnnclassifier_pa_t_kernel(tc, h1_bytes, h1_scale, W_ih1, b_ih1, b_hh1, 
 
         def moments(c):
             n = SIZES[c]
-            nm[c] = stat.tile([P, 4], F32, name="nm")
             rs[c] = stat.tile([P, 4], F32, name="rs")
             nc.scalar.activation(out=rs[c][:, :n], in_=sq[c][:, :n], func=ACT.Copy, scale=1.0 / H**3, bias=EPS)
-            nc.scalar.activation(out=nm[c][:, :n], in_=sm[c][:, :n], func=ACT.Copy, scale=-1.0 / H)
 
         def inv_root(c):
             n = SIZES[c]
             nc.gpsimd.tensor_tensor(out=rs[c][:, :n], in0=rs[c][:, :n], in1=half[:, :n], op=ALU.pow)
 
+        def shift(c):
+            n = SIZES[c]
+            nm[c] = stat.tile([P, 4], F32, name="nm")
+            nc.vector.scalar_tensor_tensor(out=nm[c][:, :n], in0=sm[c][:, :n], scalar=-1.0 / H, in1=rs[c][:, :n], op0=ALU.mult, op1=ALU.mult)
+
+        def by_diagonal(c, j):
+            return j % 2 == 0
+
         def normalise(c, j):
-            zz[c, j] = work.tile([P, H], F32, name="zz", bufs=8)
+            if by_diagonal(c, j):
+                zz[c, j] = work.tile([P, P], F32, name="diag", bufs=4)
+                nc.vector.tensor_scalar(out=zz[c, j][:], in0=ident[:], scalar1=rs[c][:, j : j + 1], scalar2=None, op0=ALU.mult)
+                return
+            zz[c, j] = work.tile([P, H], F32, name="zz", bufs=4)
             nc.vector.tensor_scalar(
-                out=zz[c, j][:], in0=hh[c, j][:], scalar1=nm[c][:, j : j + 1], scalar2=rs[c][:, j : j + 1], op0=ALU.add, op1=ALU.mult
+                out=zz[c, j][:], in0=hh[c, j][:], scalar1=rs[c][:, j : j + 1], scalar2=nm[c][:, j : j + 1], op0=ALU.mult, op1=ALU.add
             )
 
         def turn_z(c, t):
             fmb[c, t] = ps_f.tile([P, SIZES[c] * P], F32, name="fm")
             for j in range(SIZES[c]):
-                nc.tensor.transpose(fmb[c, t][:, j * P : (j + 1) * P], zz[c, j][:, t * P : (t + 1) * P], ident[:])
+                dst = fmb[c, t][:, j * P : (j + 1) * P]
+                if by_diagonal(c, j):
+                    nc.tensor.matmul(dst, lhsT=hh[c, j][:, t * P : (t + 1) * P], rhs=zz[c, j][:], start=True, stop=False)
+                    nc.tensor.matmul(dst, lhsT=nm[c][:, j : j + 1].to_broadcast([P, P]), rhs=ident[:], start=False, stop=True, is_transpose=True)
+                else:
+                    nc.tensor.transpose(dst, zz[c, j][:, t * P : (t + 1) * P], ident[:])
 
         def on_vector(c, t):
             return t == 3 and nch - 4 <= c < nch - 2
@@ -195,7 +210,7 @@ def tile_rnnclassifier_pa_t_kernel(tc, h1_bytes, h1_scale, W_ih1, b_ih1, b_hh1, 
 
         def pool_share(c):
             if c < nch - 5:
-                return SIZES[c] * P * 3 // 4
+                return SIZES[c] * P * 11 // 16
             return SIZES[c] * P // 4 if c <= nch - 4 else 0
 
         def weave_pool(c):
@@ -309,6 +324,7 @@ def tile_rnnclassifier_pa_t_kernel(tc, h1_bytes, h1_scale, W_ih1, b_ih1, b_hh1, 
             on(mm2, c_out)
             on_pair(scale_out, c_quant, 0)
             on(affine, c_affine, 0)
+            on(moments, c_norm)
             on(inv_root, c_norm)
             on_tile(add_bias, c_tanh, 0)
             on_tile(mm1, c_tanh, 2)
@@ -327,6 +343,7 @@ def tile_rnnclassifier_pa_t_kernel(tc, h1_bytes, h1_scale, W_ih1, b_ih1, b_hh1, 
                 on_tile(tanh, c_tanh, j)
             if on_vector(c_affine, 3):
                 affine(c_affine, 3)
+            on(shift, c_norm)
             on(quant_x, c_quant)
             if i == 1:
                 first_weights_quantised()
@@ -339,11 +356,10 @@ def tile_rnnclassifier_pa_t_kernel(tc, h1_bytes, h1_scale, W_ih1, b_ih1, b_hh1, 
                 on(affine, c_affine, 3)
             for j in range(4):
                 on_tile(square, c_tanh, j)
-            on(moments, c_tanh)
-            for t in range(3):
-                on(turn_z, c_norm, t)
             on_tile(mm1, c_quant, 0)
             on_tile(mm1, c_quant, 1)
+            for t in range(3):
+                on(turn_z, c_norm, t)
             if i == 2:
                 late_constants()
             if i == 3:
@@ -353,6 +369,7 @@ def tile_rnnclassifier_pa_t_kernel(tc, h1_bytes, h1_scale, W_ih1, b_ih1, b_hh1, 
         weave_pool(last - 3)
         mm2(last - 4)
         affine(last - 2, 0)
+        moments(last - 1)
         inv_root(last - 1)
         turn_z(last - 2, 3)
         for j in range(SIZES[last]):
@@ -367,9 +384,11 @@ def tile_rnnclassifier_pa_t_kernel(tc, h1_bytes, h1_scale, W_ih1, b_ih1, b_hh1, 
         affine(last - 2, 2)
         moments(last)
         inv_root(last)
+        shift(last - 1)
+        weave_vector(last - 3)
         for j in range(4):
             normalise(last - 1, j)
-        weave_vector(last - 3)
+        shift(last)
         for j in range(SIZES[last]):
             normalise(last, j)
         quant_y(last - 3)

@@ -9,7 +9,7 @@ T = 4
 EPS = 1e-5
 FLOPS = 2 * B * H * H + 2 * B * H2 * D_OUT
 SIZES = [2] + [4] * 15 + [2]
-CAST_ON_SCALAR = (2, 3)
+CAST_ON_POOL = (3, 4, 5, 6)
 
 F32 = mybir.dt.float32
 BF16 = mybir.dt.bfloat16
@@ -82,11 +82,12 @@ def tile_rnnclassifier_pa_t_kernel(tc, h1_bytes, h1_scale, W_ih1, b_ih1, b_hh1, 
         b_raw = const.tile([P, 2, T], BF16)
         nc.sync.dma_start(out=b_raw[:], in_=ln_b.rearrange("(o p t) -> p o t", o=2, t=T))
         nc.sync.dma_start(out=row_f[0:1, :], in_=fc_b.rearrange("(o k) -> o k", o=1))
-        scale = const.tile([P, 2 * P, T], F32)
+        warm = const.tile([P, 1], F32)
+        nc.scalar.activation(out=warm[:], in_=half[:, 0:1], func=ACT.Tanh)
         bias = const.tile([P, H], F32)
         g_col = const.tile([P, 2, T], F32)
         b_col = const.tile([P, 2, T], F32)
-        fcb = const.tile([P, 4, D_OUT], F32)
+        fcb = const.tile([P, D_OUT], F32)
 
         w_grp = const.tile([P, H, T], BF16, align_bytes=64)
         w_codes = const.tile([P, H], U32, align_bytes=64)
@@ -100,8 +101,8 @@ def tile_rnnclassifier_pa_t_kernel(tc, h1_bytes, h1_scale, W_ih1, b_ih1, b_hh1, 
 
         def cast(c):
             hx[c] = work.tile([P, SIZES[c] * H], BF16, name="hx", align_bytes=64)
-            if c in CAST_ON_SCALAR:
-                nc.scalar.copy(out=hx[c][:], in_=xb[c][:].bitcast(FP8))
+            if c in CAST_ON_POOL:
+                nc.gpsimd.tensor_copy(out=hx[c][:], in_=xb[c][:].bitcast(FP8))
             else:
                 nc.vector.tensor_copy(out=hx[c][:], in_=xb[c][:].bitcast(FP8))
 
@@ -121,7 +122,7 @@ def tile_rnnclassifier_pa_t_kernel(tc, h1_bytes, h1_scale, W_ih1, b_ih1, b_hh1, 
             nc.vector.tensor_tensor(
                 out=xg[c][:, h * 2 * P : h * 2 * P + n, :].rearrange("p n (u e) -> p n u e", e=2),
                 in0=xtb[c, h][:].bitcast(BF16).rearrange("p u (n e) -> p n u e", e=2),
-                in1=scale[:, :n, :].rearrange("p n (u e) -> p n u e", e=2),
+                in1=s4[:].rearrange("p (u e) -> p u e", e=2).unsqueeze(1).to_broadcast([P, n, 2, 2]),
                 op=ALU.mult,
             )
 
@@ -173,7 +174,7 @@ def tile_rnnclassifier_pa_t_kernel(tc, h1_bytes, h1_scale, W_ih1, b_ih1, b_hh1, 
             nc.vector.scalar_tensor_tensor(out=nm[c][:, :n], in0=sm[c][:, :n], scalar=-1.0 / H, in1=rs[c][:, :n], op0=ALU.mult, op1=ALU.mult)
 
         def by_diagonal(c, j):
-            return j % 2 == 0
+            return j % 2 == 0 or c == nch - 1
 
         def normalise(c, j):
             if by_diagonal(c, j):
@@ -196,7 +197,7 @@ def tile_rnnclassifier_pa_t_kernel(tc, h1_bytes, h1_scale, W_ih1, b_ih1, b_hh1, 
                     nc.tensor.transpose(dst, zz[c, j][:, t * P : (t + 1) * P], ident[:])
 
         def on_vector(c, t):
-            return t == 3 and nch - 4 <= c < nch - 2
+            return t == 0 and nch - 4 <= c < nch - 2
 
         def affine(c, t):
             if c not in yy:
@@ -209,9 +210,9 @@ def tile_rnnclassifier_pa_t_kernel(tc, h1_bytes, h1_scale, W_ih1, b_ih1, b_hh1, 
                     nc.scalar.activation(out=yy[c][:, o, t, :], in_=fmb[c, t][:], func=ACT.Identity, scale=gain, bias=shift)
 
         def pool_share(c):
-            if c < nch - 5:
+            if c < nch - 4:
                 return SIZES[c] * P * 11 // 16
-            return SIZES[c] * P // 4 if c <= nch - 4 else 0
+            return SIZES[c] * P * 5 // 16 if c == nch - 4 else 0
 
         def weave_pool(c):
             n = SIZES[c] * P
@@ -263,7 +264,7 @@ def tile_rnnclassifier_pa_t_kernel(tc, h1_bytes, h1_scale, W_ih1, b_ih1, b_hh1, 
         def finish(c):
             n = SIZES[c]
             osb[c] = work.tile([P, n, D_OUT], F32, name="osb")
-            nc.vector.tensor_tensor(out=osb[c][:], in0=ob[c][:], in1=fcb[:, :n, :], op=ALU.add)
+            nc.vector.tensor_tensor(out=osb[c][:], in0=ob[c][:], in1=fcb[:].unsqueeze(1).to_broadcast([P, n, D_OUT]), op=ALU.add)
             nc.sync.dma_start(out=rows(out, c), in_=osb[c][:])
 
         def turn_weights(pieces, grp):
@@ -289,9 +290,8 @@ def tile_rnnclassifier_pa_t_kernel(tc, h1_bytes, h1_scale, W_ih1, b_ih1, b_hh1, 
             nc.gpsimd.tensor_copy(out=g_col[:], in_=g_raw[:])
             nc.gpsimd.tensor_copy(out=b_col[:], in_=b_raw[:])
             fk = ps_f.tile([P, 4 * P], F32, name="fm")
-            for j in range(4):
-                nc.tensor.matmul(fk[:, j * P : (j + 1) * P], lhsT=ones[:], rhs=row_f[:], start=True, stop=True)
-            nc.scalar.copy(out=fcb[:].rearrange("p j f -> p (j f)"), in_=fk[:])
+            nc.tensor.matmul(fk[:, :D_OUT], lhsT=ones[:], rhs=row_f[:], start=True, stop=True)
+            nc.scalar.copy(out=fcb[:], in_=fk[:, :D_OUT])
             fw = words(f_sb[:])
             turn_weights([fw[:, 256 * o : 256 * (o + 1)] for o in range(2)], f_grp[:])
 
@@ -312,7 +312,6 @@ def tile_rnnclassifier_pa_t_kernel(tc, h1_bytes, h1_scale, W_ih1, b_ih1, b_hh1, 
 
         first_weights(0)
         cast(0)
-        nc.vector.tensor_copy(out=scale[:], in_=s4[:].unsqueeze(1).to_broadcast([P, 2 * P, T]))
         turn_x(0, 0)
         first_weights(1)
         first_bias()
@@ -320,6 +319,8 @@ def tile_rnnclassifier_pa_t_kernel(tc, h1_bytes, h1_scale, W_ih1, b_ih1, b_hh1, 
         for i in range(1, nch + 1):
             c_cast, c_turn, c_quant, c_tanh, c_norm, c_affine, c_weave, c_out = range(i + 1, i - 7, -1)
             on(load, i + 2)
+            if c_cast in CAST_ON_POOL:
+                cast(c_cast)
             on(weave_pool, c_weave)
             on(mm2, c_out)
             on_pair(scale_out, c_quant, 0)
@@ -341,8 +342,6 @@ def tile_rnnclassifier_pa_t_kernel(tc, h1_bytes, h1_scale, W_ih1, b_ih1, b_hh1, 
             on_tile(add_bias, c_tanh, 3)
             for j in range(4):
                 on_tile(tanh, c_tanh, j)
-            if on_vector(c_affine, 3):
-                affine(c_affine, 3)
             on(shift, c_norm)
             on(quant_x, c_quant)
             if i == 1:
@@ -350,10 +349,10 @@ def tile_rnnclassifier_pa_t_kernel(tc, h1_bytes, h1_scale, W_ih1, b_ih1, b_hh1, 
             for j in range(4):
                 on_tile(normalise, c_norm, j)
             on(weave_vector, c_weave)
-            on(cast, c_cast)
+            if c_cast not in CAST_ON_POOL:
+                on(cast, c_cast)
             on(quant_y, c_weave)
-            if not on_vector(c_affine, 3):
-                on(affine, c_affine, 3)
+            on(affine, c_affine, 3)
             for j in range(4):
                 on_tile(square, c_tanh, j)
             on_tile(mm1, c_quant, 0)
@@ -368,26 +367,26 @@ def tile_rnnclassifier_pa_t_kernel(tc, h1_bytes, h1_scale, W_ih1, b_ih1, b_hh1, 
         last = nch - 1
         weave_pool(last - 3)
         mm2(last - 4)
+        for j in range(SIZES[last]):
+            add_bias(last, j)
         affine(last - 2, 0)
         moments(last - 1)
         inv_root(last - 1)
         turn_z(last - 2, 3)
-        for j in range(SIZES[last]):
-            add_bias(last, j)
         finish(last - 4)
         for j in range(SIZES[last]):
             tanh(last, j)
-        affine(last - 2, 3)
         affine(last - 2, 1)
         for j in range(SIZES[last]):
             square(last, j)
         affine(last - 2, 2)
         moments(last)
-        inv_root(last)
+        affine(last - 2, 3)
         shift(last - 1)
-        weave_vector(last - 3)
         for j in range(4):
             normalise(last - 1, j)
+        inv_root(last)
+        weave_vector(last - 3)
         shift(last)
         for j in range(SIZES[last]):
             normalise(last, j)

@@ -8,8 +8,6 @@ P = 128
 T = 4
 EPS = 1e-5
 FLOPS = 2 * B * H * H + 2 * B * H2 * D_OUT
-SIZES = [2] + [4] * 15 + [2]
-CAST_ON_POOL = (3, 4, 5, 6)
 
 F32 = mybir.dt.float32
 BF16 = mybir.dt.bfloat16
@@ -19,6 +17,13 @@ FP8 = mybir.dt.float8_e4m3fn
 FP8X4 = mybir.dt.float8_e4m3fn_x4
 ACT = mybir.ActivationFunctionType
 ALU = mybir.AluOpType
+SIZES = [4] * 16
+HH_BUFS = 8
+X, S1, FM, HT = 0, 1, 2, 4
+TILES = 4
+PARTS = {"a": (15, 0, 2), "b": (15, 2, 2)}
+HX_BUFS = 6
+XB_BUFS = 5
 
 
 def tile_rnnclassifier_pa_t_kernel(tc, h1_bytes, h1_scale, W_ih1, b_ih1, b_hh1, ln_g, ln_b, fc_W, fc_b, out):
@@ -34,31 +39,29 @@ def tile_rnnclassifier_pa_t_kernel(tc, h1_bytes, h1_scale, W_ih1, b_ih1, b_hh1, 
         const = ctx.enter_context(tc.tile_pool(name="const", bufs=1))
         work = ctx.enter_context(tc.tile_pool(name="work", bufs=2))
         stat = ctx.enter_context(tc.tile_pool(name="stat", bufs=3))
-        ps_x = ctx.enter_context(tc.psum_pool(name="ps_x", bufs=2))
-        ps_s = ctx.enter_context(tc.psum_pool(name="ps_s", bufs=2))
-        ps_f = ctx.enter_context(tc.psum_pool(name="ps_f", bufs=3))
-        ps_o = ctx.enter_context(tc.psum_pool(name="ps_o", bufs=1))
+        psum = ctx.enter_context(tc.psum_pool(name="psum", bufs=1))
         ctx.enter_context(tc.manual_schedule())
 
         xb, hx, xg, xc, xs = {}, {}, {}, {}, {}
-        hb, hh, zz, sm, nm, sq, rs = {}, {}, {}, {}, {}, {}, {}
+        hh, ht, zz, bn, mv, rs, nm = {}, {}, {}, {}, {}, {}, {}
         yy, yg, yc, ys = {}, {}, {}, {}
         osb, fmb, xtb, s1b, ob = {}, {}, {}, {}, {}
 
-        def load(c):
-            xb[c] = work.tile([P, SIZES[c] * H], U8, name="x_bytes", align_bytes=64, bufs=4)
-            nc.sync.dma_start(out=xb[c][:].rearrange("p (j k) -> p j k", k=H), in_=rows(h1_bytes, c))
+        def load(c, h=None):
+            j0, m = (0, TILES) if h is None else (2 * h, 2)
+            raw = work.tile([P, m * H], U8, name="x_bytes", align_bytes=64, bufs=XB_BUFS)
+            nc.sync.dma_start(out=raw[:].rearrange("p (j k) -> p j k", k=H), in_=rows(h1_bytes, c)[:, j0 : j0 + m, :])
+            for g in range(m // 2):
+                xb[c, j0 // 2 + g] = raw[:, 2 * g * H : 2 * (g + 1) * H]
 
-        row_b = const.tile([P, H], BF16)
-        nc.vector.memset(row_b[:], 0.0)
-        row_f = const.tile([P, D_OUT], BF16)
-        nc.vector.memset(row_f[:], 0.0)
-        ones = const.tile([P, P], BF16)
-        nc.vector.memset(ones[:], 1.0)
-        ident = const.tile([P, P], F32)
+        ident = const.tile([P, P], F32, name="ident")
         make_identity(nc, ident[:])
-        half = const.tile([P, 4], F32)
+        half = const.tile([P, 4], F32, name="half")
         nc.gpsimd.memset(half[:], -0.5)
+
+        mvs = const.tile([P, nch, 4, 3], F32, name="mvs")
+        nc.gpsimd.memset(mvs[:], 1.0)
+        nc.gpsimd.tensor_scalar(out=mvs[:], in0=mvs[:], scalar1=EPS, scalar2=0.0, op0=ALU.mult, op1=ALU.add)
 
         w_sb = {}
 
@@ -66,52 +69,58 @@ def tile_rnnclassifier_pa_t_kernel(tc, h1_bytes, h1_scale, W_ih1, b_ih1, b_hh1, 
             w_sb[h] = const.tile([P, 2, H], BF16, name="w_sb%d" % h)
             nc.sync.dma_start(out=w_sb[h][:], in_=W_ih1.rearrange("(m t) k -> m t k", t=T)[:, 2 * h : 2 * h + 2, :])
 
+        load(0, 0)
         load_w(0)
-        load(0)
-        s4 = const.tile([P, T], F32)
-        nc.sync.dma_start(out=s4[:], in_=h1_scale.rearrange("o (p t) -> p (o t)", t=T))
+        load(0, 1)
         load_w(1)
-        nc.scalar.dma_start(out=row_b[0:1, :], in_=b_ih1.rearrange("(o k) -> o k", o=1))
-        nc.scalar.dma_start(out=row_b[1:2, :], in_=b_hh1.rearrange("(o k) -> o k", o=1))
+        s4 = const.tile([P, T], F32, name="s4")
+        nc.sync.dma_start(out=s4[:], in_=h1_scale.rearrange("o (p t) -> p (o t)", t=T))
         load(1)
+        bi_raw = const.tile([P, T], BF16, name="bi_raw")
+        nc.sync.dma_start(out=bi_raw[:], in_=b_ih1.rearrange("(p t) -> p t", t=T))
+        bh_raw = const.tile([P, T], BF16, name="bh_raw")
+        nc.sync.dma_start(out=bh_raw[:], in_=b_hh1.rearrange("(p t) -> p t", t=T))
         load(2)
-        f_sb = const.tile([P, H2], BF16)
+        load(3)
+        f_sb = const.tile([P, H2], BF16, name="f_sb")
         nc.sync.dma_start(out=f_sb[:], in_=fc_W)
-        g_raw = const.tile([P, 2, T], BF16)
+        g_raw = const.tile([P, 2, T], BF16, name="g_raw")
         nc.sync.dma_start(out=g_raw[:], in_=ln_g.rearrange("(o p t) -> p o t", o=2, t=T))
-        b_raw = const.tile([P, 2, T], BF16)
+        b_raw = const.tile([P, 2, T], BF16, name="b_raw")
         nc.sync.dma_start(out=b_raw[:], in_=ln_b.rearrange("(o p t) -> p o t", o=2, t=T))
-        nc.sync.dma_start(out=row_f[0:1, :], in_=fc_b.rearrange("(o k) -> o k", o=1))
-        warm = const.tile([P, 1], F32)
-        nc.scalar.activation(out=warm[:], in_=half[:, 0:1], func=ACT.Tanh)
-        bias = const.tile([P, H], F32)
-        g_col = const.tile([P, 2, T], F32)
-        b_col = const.tile([P, 2, T], F32)
-        fcb = const.tile([P, D_OUT], F32)
+        fb_raw = const.tile([P, 1], BF16, name="fb_raw")
+        nc.sync.dma_start(out=fb_raw[:], in_=fc_b.rearrange("(p o) -> p o", o=1))
+        fb_col = const.tile([P, 1], F32, name="fb_col")
+        bias = const.tile([P, T], F32, name="bias")
+        g_col = const.tile([P, 2, T], F32, name="g_col")
+        b_col = const.tile([P, 2, T], F32, name="b_col")
+        fcb = const.tile([P, D_OUT], F32, name="fcb")
 
-        w_grp = const.tile([P, H, T], BF16, align_bytes=64)
-        w_codes = const.tile([P, H], U32, align_bytes=64)
-        w_scales = const.tile([P, H], U8, align_bytes=64)
-        f_grp = const.tile([P, 2 * D_OUT, T], BF16, align_bytes=64)
-        f_codes = const.tile([P, 2 * D_OUT], U32, align_bytes=64)
-        f_scales = const.tile([P, 2 * D_OUT], U8, align_bytes=64)
+        w_grp = const.tile([P, H, T], BF16, align_bytes=64, name="w_grp")
+        w_codes = const.tile([P, H], U32, align_bytes=64, name="w_codes")
+        w_scales = const.tile([P, H], U8, align_bytes=64, name="w_scales")
+        f_grp = const.tile([P, 2 * D_OUT, T], BF16, align_bytes=64, name="f_grp")
+        f_codes = const.tile([P, 2 * D_OUT], U32, align_bytes=64, name="f_codes")
+        f_scales = const.tile([P, 2 * D_OUT], U8, align_bytes=64, name="f_scales")
 
         def words(ap):
             return ap.bitcast(F32)
 
-        def cast(c):
-            hx[c] = work.tile([P, SIZES[c] * H], BF16, name="hx", align_bytes=64)
-            if c in CAST_ON_POOL:
-                nc.gpsimd.tensor_copy(out=hx[c][:], in_=xb[c][:].bitcast(FP8))
+        def cast(c, h, eng):
+            hx[c, h] = work.tile([P, 2 * H], BF16, name="hx", align_bytes=64, bufs=HX_BUFS)
+            if eng is nc.scalar:
+                nc.scalar.copy(out=hx[c, h][:], in_=xb[c, h].bitcast(FP8))
             else:
-                nc.vector.tensor_copy(out=hx[c][:], in_=xb[c][:].bitcast(FP8))
+                eng.tensor_copy(out=hx[c, h][:], in_=xb[c, h].bitcast(FP8))
 
-        def turn_x(c, h):
+        def bank(k, shape):
+            return psum.tile(shape, F32, name="bank%d" % k)
+
+        def turn_x(c, h, kind=X):
             m = min(2, SIZES[c] - 2 * h)
-            xtb[c, h] = ps_x.tile([P, 2, m * P], F32, name="xt")
+            xtb[c, h] = bank(kind, [P, 2, m * P])
             for jj in range(m):
-                j = 2 * h + jj
-                w = words(hx[c][:, j * H : (j + 1) * H])
+                w = words(hx[c, h][:, jj * H : (jj + 1) * H])
                 for u in range(2):
                     nc.tensor.transpose(xtb[c, h][:, u, jj * P : (jj + 1) * P], w[:, u : H // 2 : 2], ident[:])
 
@@ -132,37 +141,46 @@ def tile_rnnclassifier_pa_t_kernel(tc, h1_bytes, h1_scale, W_ih1, b_ih1, b_hh1, 
             xs[c] = work.tile([P, n], U8, name="xs", align_bytes=64)
             nc.vector.quantize_mx(out=xc[c][:].bitcast(FP8X4), scales=xs[c][:], in_=xg[c][:].rearrange("p n t -> p (n t)"))
 
-        def mm1(c, j):
-            s1b[c, j] = ps_s.tile([P, H], F32, name="s1")
+        def mm1(c, t, kind=S1):
+            s1b[c, t] = bank(kind, [P, SIZES[c] * P])
             nc.tensor.matmul_mx(
-                out=s1b[c, j][:],
-                lhsT=xc[c][:, j * P : (j + 1) * P].bitcast(FP8X4),
-                lhsT_scale=xs[c][:, j * P : (j + 1) * P],
-                rhs=w_codes[:].bitcast(FP8X4),
-                rhs_scale=w_scales[:],
+                out=s1b[c, t][:],
+                lhsT=w_codes[:, t * P : (t + 1) * P].bitcast(FP8X4),
+                lhsT_scale=w_scales[:, t * P : (t + 1) * P],
+                rhs=xc[c][:].bitcast(FP8X4),
+                rhs_scale=xs[c][:],
                 start=True,
                 stop=True,
             )
 
-        def add_bias(c, j):
-            hb[c, j] = work.tile([P, H], F32, name="hb", bufs=4)
-            nc.vector.tensor_tensor(out=hb[c, j][:], in0=s1b[c, j][:], in1=bias[:], op=ALU.add)
+        def tanh(c, t):
+            hh[c, t] = work.tile([P, SIZES[c] * P], F32, name="hh", bufs=HH_BUFS)
+            nc.scalar.activation(out=hh[c, t][:], in_=s1b[c, t][:], func=ACT.Tanh, bias=bias[:, t : t + 1])
 
-        def tanh(c, j):
-            if c not in sm:
-                sm[c] = stat.tile([P, 4], F32, name="sm")
-                sq[c] = stat.tile([P, 4], F32, name="sq")
-            hh[c, j] = work.tile([P, H], F32, name="hh", bufs=12)
-            nc.scalar.activation(out=hh[c, j][:], in_=hb[c, j][:], func=ACT.Tanh, accum_out=sm[c][:, j : j + 1])
+        def turn(dst, src, plain):
+            if plain:
+                nc.tensor.matmul(dst, lhsT=src, rhs=ident[:], start=True, stop=True)
+            else:
+                nc.tensor.transpose(dst, src, ident[:])
 
-        def square(c, j):
-            junk = work.tile([P, H], BF16, name="junk")
-            nc.scalar.activation(out=junk[:], in_=hh[c, j][:], func=ACT.Square, scale=-float(H), bias=sm[c][:, j : j + 1], accum_out=sq[c][:, j : j + 1])
+        def turn_h(c, j, plain=0, kind=None):
+            ht[c, j] = bank(HT + j if kind is None else kind, [P, H])
+            for t in range(T):
+                turn(ht[c, j][:, t * P : (t + 1) * P], hh[c, t][:, j * P : (j + 1) * P], t < plain)
 
-        def moments(c):
+        def stats(c, j):
+            bn[c, j] = stat.tile([P, 6], F32, name="bn", bufs=4)
+            nc.vector.bn_stats(out=bn[c, j][:], in_=ht[c, j][:])
+
+        def moments(c, j):
+            if c not in mv:
+                mv[c] = mvs[:, c]
+            nc.vector.bn_aggr(out=mv[c][:, j, 0:2], in_=bn[c, j][:])
+
+        def add_eps(c):
             n = SIZES[c]
             rs[c] = stat.tile([P, 4], F32, name="rs")
-            nc.scalar.activation(out=rs[c][:, :n], in_=sq[c][:, :n], func=ACT.Copy, scale=1.0 / H**3, bias=EPS)
+            nc.vector.tensor_reduce(out=rs[c][:, :n], in_=mv[c][:, :n, 1:3], axis=mybir.AxisListType.X, op=ALU.add)
 
         def inv_root(c):
             n = SIZES[c]
@@ -171,104 +189,76 @@ def tile_rnnclassifier_pa_t_kernel(tc, h1_bytes, h1_scale, W_ih1, b_ih1, b_hh1, 
         def shift(c):
             n = SIZES[c]
             nm[c] = stat.tile([P, 4], F32, name="nm")
-            nc.vector.scalar_tensor_tensor(out=nm[c][:, :n], in0=sm[c][:, :n], scalar=-1.0 / H, in1=rs[c][:, :n], op0=ALU.mult, op1=ALU.mult)
+            nc.vector.scalar_tensor_tensor(out=nm[c][:, :n], in0=mv[c][:, :n, 0], scalar=-1.0, in1=rs[c][:, :n], op0=ALU.mult, op1=ALU.mult)
 
-        def by_diagonal(c, j):
-            return j % 2 == 0 or c == nch - 1
-
-        def normalise(c, j):
-            if by_diagonal(c, j):
-                zz[c, j] = work.tile([P, P], F32, name="diag", bufs=4)
-                nc.vector.tensor_scalar(out=zz[c, j][:], in0=ident[:], scalar1=rs[c][:, j : j + 1], scalar2=None, op0=ALU.mult)
-                return
-            zz[c, j] = work.tile([P, H], F32, name="zz", bufs=4)
-            nc.vector.tensor_scalar(
-                out=zz[c, j][:], in0=hh[c, j][:], scalar1=rs[c][:, j : j + 1], scalar2=nm[c][:, j : j + 1], op0=ALU.mult, op1=ALU.add
-            )
-
-        def turn_z(c, t):
-            fmb[c, t] = ps_f.tile([P, SIZES[c] * P], F32, name="fm")
-            for j in range(SIZES[c]):
-                dst = fmb[c, t][:, j * P : (j + 1) * P]
-                if by_diagonal(c, j):
-                    nc.tensor.matmul(dst, lhsT=hh[c, j][:, t * P : (t + 1) * P], rhs=zz[c, j][:], start=True, stop=False)
-                    nc.tensor.matmul(dst, lhsT=nm[c][:, j : j + 1].to_broadcast([P, P]), rhs=ident[:], start=False, stop=True, is_transpose=True)
-                else:
-                    nc.tensor.transpose(dst, zz[c, j][:, t * P : (t + 1) * P], ident[:])
-
-        def on_vector(c, t):
-            return t == 0 and nch - 4 <= c < nch - 2
-
-        def affine(c, t):
-            if c not in yy:
-                yy[c] = work.tile([P, 2, T, SIZES[c] * P], BF16, name="yy", bufs=3)
-            for o in range(2):
-                gain, shift = g_col[:, o, t : t + 1], b_col[:, o, t : t + 1]
-                if on_vector(c, t):
-                    nc.vector.tensor_scalar(out=yy[c][:, o, t, :], in0=fmb[c, t][:], scalar1=gain, scalar2=shift, op0=ALU.mult, op1=ALU.add)
-                else:
-                    nc.scalar.activation(out=yy[c][:, o, t, :], in_=fmb[c, t][:], func=ACT.Identity, scale=gain, bias=shift)
-
-        def pool_share(c):
-            if c < nch - 4:
-                return SIZES[c] * P * 11 // 16
-            return SIZES[c] * P * 5 // 16 if c == nch - 4 else 0
-
-        def weave_pool(c):
-            n = SIZES[c] * P
-            yg[c] = work.tile([P, 2, n, T], BF16, name="yg", align_bytes=64, bufs=1)
-            m = pool_share(c)
-            if m == 0:
-                return
-            nc.gpsimd.tensor_scalar(
-                out=yg[c][:, :, :m, :], in0=yy[c][:, :, :, :m].rearrange("p o t n -> p o n t"), scalar1=1.0, scalar2=0.0, op0=ALU.mult, op1=ALU.add
-            )
-
-        def weave_vector(c):
-            m = pool_share(c)
-            nc.vector.tensor_copy(
-                out=yg[c][:, :, m:, :].rearrange("p o (n i) t -> p o n t i", i=4),
-                in_=yy[c][:, :, :, m:].rearrange("p o t (n i) -> p o n t i", i=4),
-            )
-
-        def weave_scalar(c):
-            yg[c] = work.tile([P, 2, SIZES[c] * P, T], BF16, name="yg_last", align_bytes=64, bufs=1)
-            for o in range(2):
-                nc.scalar.copy(out=yg[c][:, o].rearrange("p (n i) t -> p n t i", i=4), in_=yy[c][:, o].rearrange("p t (n i) -> p n t i", i=4))
-
-        def quant_y(c):
-            n = SIZES[c] * P
-            yc[c] = work.tile([P, 2 * n], U32, name="yc", align_bytes=64)
-            ys[c] = work.tile([P, 2 * n], U8, name="ys", align_bytes=64)
-            nc.vector.quantize_mx(out=yc[c][:].bitcast(FP8X4), scales=ys[c][:], in_=yg[c][:].rearrange("p o n t -> p (o n t)"))
-
-        def mm2(c):
-            n = SIZES[c] * P
-            if c == nch - 1:
-                ob[c] = ps_x.tile([P, SIZES[c], D_OUT], F32, name="xt")
+        def normalise(c, j, eng):
+            zz[c, j] = work.tile([P, H], F32, name="zz", bufs=8)
+            rstd = rs[c][:, j : j + 1]
+            if eng is nc.vector:
+                nc.vector.tensor_scalar(out=zz[c, j][:], in0=ht[c, j][:], scalar1=mv[c][:, j, 0:1], scalar2=rstd, op0=ALU.subtract, op1=ALU.mult)
             else:
-                ob[c] = ps_o.tile([P, SIZES[c], D_OUT], F32, name="ob")
-            for j in range(SIZES[c]):
+                nc.scalar.activation(out=zz[c, j][:], in_=ht[c, j][:], func=ACT.Identity, scale=rstd, bias=nm[c][:, j : j + 1])
+
+        def tiles(u):
+            return PARTS.get(u, (u, 0, TILES))
+
+        def turn_z(u, t, plain=0, kind=None):
+            c, j0, m = tiles(u)
+            fmb[u, t] = bank(FM + t % 2 if kind is None else kind, [P, m * P])
+            for j in range(m):
+                turn(fmb[u, t][:, j * P : (j + 1) * P], zz[c, j0 + j][:, t * P : (t + 1) * P], j < plain)
+
+        def affine(u, t, o, eng):
+            if u not in yy:
+                yy[u] = work.tile([P, 2, T, tiles(u)[2] * P], BF16, name="yy", bufs=3)
+            gain, offset = g_col[:, o, t : t + 1], b_col[:, o, t : t + 1]
+            if eng is nc.vector:
+                nc.vector.tensor_scalar(out=yy[u][:, o, t, :], in0=fmb[u, t][:], scalar1=gain, scalar2=offset, op0=ALU.mult, op1=ALU.add)
+            else:
+                nc.scalar.activation(out=yy[u][:, o, t, :], in_=fmb[u, t][:], func=ACT.Identity, scale=gain, bias=offset)
+
+        def weave(u, lo, hi, eng):
+            if u not in yg:
+                yg[u] = work.tile([P, 2, tiles(u)[2] * P, T], BF16, name="yg_end" if u in PARTS else "yg", align_bytes=64, bufs=2 if u in PARTS else 1)
+            dst, src = yg[u][:, :, lo:hi, :], yy[u][:, :, :, lo:hi]
+            if eng is nc.gpsimd:
+                nc.gpsimd.tensor_scalar(out=dst, in0=src.rearrange("p o t n -> p o n t"), scalar1=1.0, scalar2=0.0, op0=ALU.mult, op1=ALU.add)
+            elif eng is nc.vector:
+                nc.vector.tensor_copy(out=dst.rearrange("p o (n i) t -> p o n t i", i=4), in_=src.rearrange("p o t (n i) -> p o n t i", i=4))
+            else:
                 for o in range(2):
-                    cols = slice(o * n + j * P, o * n + (j + 1) * P)
+                    nc.scalar.copy(out=dst[:, o].rearrange("p (n i) t -> p n t i", i=4), in_=src[:, o].rearrange("p t (n i) -> p n t i", i=4))
+
+        def quant_y(u):
+            n = tiles(u)[2] * P
+            yc[u] = work.tile([P, 2 * n], U32, name="yc", align_bytes=64)
+            ys[u] = work.tile([P, 2 * n], U8, name="ys", align_bytes=64)
+            nc.vector.quantize_mx(out=yc[u][:].bitcast(FP8X4), scales=ys[u][:], in_=yg[u][:].rearrange("p o n t -> p (o n t)"))
+
+        def mm2(u, kind=X):
+            m = tiles(u)[2]
+            ob[u] = bank(kind, [P, m, D_OUT])
+            for j in range(m):
+                for o in range(2):
+                    cols = slice((o * m + j) * P, (o * m + j + 1) * P)
                     nc.tensor.matmul_mx(
-                        out=ob[c][:, j, :],
-                        lhsT=yc[c][:, cols].bitcast(FP8X4),
-                        lhsT_scale=ys[c][:, cols],
+                        out=ob[u][:, j, :],
+                        lhsT=yc[u][:, cols].bitcast(FP8X4),
+                        lhsT_scale=ys[u][:, cols],
                         rhs=f_codes[:, o * P : (o + 1) * P].bitcast(FP8X4),
                         rhs_scale=f_scales[:, o * P : (o + 1) * P],
                         start=(o == 0),
                         stop=(o == 1),
                     )
 
-        def finish(c):
-            n = SIZES[c]
-            osb[c] = work.tile([P, n, D_OUT], F32, name="osb")
-            nc.vector.tensor_tensor(out=osb[c][:], in0=ob[c][:], in1=fcb[:].unsqueeze(1).to_broadcast([P, n, D_OUT]), op=ALU.add)
-            nc.sync.dma_start(out=rows(out, c), in_=osb[c][:])
+        def finish(u):
+            c, j0, m = tiles(u)
+            osb[u] = work.tile([P, m, D_OUT], F32, name="osb", bufs=3)
+            nc.vector.tensor_tensor(out=osb[u][:], in0=ob[u][:], in1=fcb[:].unsqueeze(1).to_broadcast([P, m, D_OUT]), op=ALU.add)
+            nc.sync.dma_start(out=rows(out, c)[:, j0 : j0 + m, :], in_=osb[u][:])
 
-        def turn_weights(pieces, grp):
-            xt = ps_f.tile([P, 4 * P], F32, name="fm")
+        def turn_weights(pieces, grp, kind):
+            xt = bank(kind, [P, 4 * P])
             v = xt[:].rearrange("p (a u r) -> p a u r", a=2, u=2)
             for a in range(2):
                 for u in range(2):
@@ -276,24 +266,28 @@ def tile_rnnclassifier_pa_t_kernel(tc, h1_bytes, h1_scale, W_ih1, b_ih1, b_hh1, 
             nc.scalar.copy(out=words(grp).rearrange("p (j r) u -> p j r u", j=2), in_=v.rearrange("p j u r -> p j r u"))
 
         def first_weights(h):
-            turn_weights([words(w_sb[h][:, a, :]) for a in range(2)], w_grp[:, h * 256 : h * 256 + 256, :])
+            turn_weights([words(w_sb[h][:, a, :]) for a in range(2)], w_grp[:, h * 256 : h * 256 + 256, :], FM + h)
 
         def first_bias():
-            bk = ps_f.tile([P, 4 * P], F32, name="fm")
-            nc.tensor.matmul(bk[:], lhsT=ones[:], rhs=row_b[:], start=True, stop=True)
-            nc.scalar.copy(out=bias[:].rearrange("p (t m) -> p t m", t=T), in_=bk[:].rearrange("p (m t) -> p t m", t=T))
+            nc.gpsimd.tensor_tensor(out=bias[:], in0=bi_raw[:], in1=bh_raw[:], op=ALU.add)
 
-        def first_weights_quantised():
-            nc.vector.quantize_mx(out=w_codes[:].bitcast(FP8X4), scales=w_scales[:], in_=w_grp[:].rearrange("p n t -> p (n t)"))
+        def first_weights_quantised(h):
+            cols = slice(h * 2 * P, (h + 1) * 2 * P)
+            nc.vector.quantize_mx(out=w_codes[:, cols].bitcast(FP8X4), scales=w_scales[:, cols], in_=w_grp[:, cols, :].rearrange("p n t -> p (n t)"))
 
         def late_constants():
             nc.gpsimd.tensor_copy(out=g_col[:], in_=g_raw[:])
             nc.gpsimd.tensor_copy(out=b_col[:], in_=b_raw[:])
-            fk = ps_f.tile([P, 4 * P], F32, name="fm")
-            nc.tensor.matmul(fk[:, :D_OUT], lhsT=ones[:], rhs=row_f[:], start=True, stop=True)
-            nc.scalar.copy(out=fcb[:], in_=fk[:, :D_OUT])
+            nc.gpsimd.tensor_copy(out=fb_col[:], in_=fb_raw[:])
+
+        def late_bias():
+            fk = bank(FM, [P, D_OUT])
+            nc.tensor.transpose(fk[:], fb_col[:].to_broadcast([P, P]), ident[:])
+            nc.scalar.copy(out=fcb[:], in_=fk[:])
+
+        def late_weights():
             fw = words(f_sb[:])
-            turn_weights([fw[:, 256 * o : 256 * (o + 1)] for o in range(2)], f_grp[:])
+            turn_weights([fw[:, 256 * o : 256 * (o + 1)] for o in range(2)], f_grp[:], HT + 2)
 
         def late_weights_quantised():
             nc.vector.quantize_mx(out=f_codes[:].bitcast(FP8X4), scales=f_scales[:], in_=f_grp[:].rearrange("p n t -> p (n t)"))
@@ -302,110 +296,237 @@ def tile_rnnclassifier_pa_t_kernel(tc, h1_bytes, h1_scale, W_ih1, b_ih1, b_hh1, 
             if 0 <= c < nch:
                 fn(c, *args)
 
-        def on_tile(fn, c, j):
+        def on_tile(fn, c, j, *args):
             if 0 <= c < nch and j < SIZES[c]:
-                fn(c, j)
+                fn(c, j, *args)
 
-        def on_pair(fn, c, h):
+        def on_pair(fn, c, h, *args):
             if 0 <= c < nch and 2 * h < SIZES[c]:
-                fn(c, h)
+                fn(c, h, *args)
 
-        first_weights(0)
-        cast(0)
+        V, S, G = nc.vector, nc.scalar, nc.gpsimd
+        N = TILES * P
+        cast(0, 0, V)
         turn_x(0, 0)
+        cast(0, 1, V)
+        first_weights(0)
+        turn_x(0, 1, HT)
+        cast(1, 1, S)
         first_weights(1)
         first_bias()
-        cast(1)
-        for i in range(1, nch + 1):
-            c_cast, c_turn, c_quant, c_tanh, c_norm, c_affine, c_weave, c_out = range(i + 1, i - 7, -1)
-            on(load, i + 2)
-            if c_cast in CAST_ON_POOL:
-                cast(c_cast)
-            on(weave_pool, c_weave)
-            on(mm2, c_out)
-            on_pair(scale_out, c_quant, 0)
-            on(affine, c_affine, 0)
-            on(moments, c_norm)
-            on(inv_root, c_norm)
-            on_tile(add_bias, c_tanh, 0)
-            on_tile(mm1, c_tanh, 2)
-            on_pair(scale_out, c_quant, 1)
-            on(affine, c_affine, 1)
-            on_tile(add_bias, c_tanh, 1)
-            on_tile(mm1, c_tanh, 3)
-            on(turn_z, c_affine, 3)
-            on_pair(turn_x, c_turn, 0)
-            on_pair(turn_x, c_turn, 1)
-            on(affine, c_affine, 2)
-            on(finish, c_out)
-            on_tile(add_bias, c_tanh, 2)
-            on_tile(add_bias, c_tanh, 3)
-            for j in range(4):
-                on_tile(tanh, c_tanh, j)
-            on(shift, c_norm)
-            on(quant_x, c_quant)
-            if i == 1:
-                first_weights_quantised()
-            for j in range(4):
-                on_tile(normalise, c_norm, j)
-            on(weave_vector, c_weave)
-            if c_cast not in CAST_ON_POOL:
-                on(cast, c_cast)
-            on(quant_y, c_weave)
-            on(affine, c_affine, 3)
-            for j in range(4):
-                on_tile(square, c_tanh, j)
-            on_tile(mm1, c_quant, 0)
-            on_tile(mm1, c_quant, 1)
-            for t in range(3):
-                on(turn_z, c_norm, t)
-            if i == 2:
-                late_constants()
-            if i == 3:
-                late_weights_quantised()
+        cast(1, 0, G)
+        scale_out(0, 0)
+        scale_out(0, 1)
+        turn_x(1, 0)
+        turn_x(1, 1, HT + 1)
+        first_weights_quantised(0)
+        quant_x(0)
+        first_weights_quantised(1)
+        for t, kind in enumerate((S1, FM, FM + 1, HT + 3)):
+            mm1(0, t, kind)
+        cast(2, 0, S)
+        scale_out(1, 0)
+        turn_x(2, 0)
+        scale_out(1, 1)
+        late_constants()
+        cast(2, 1, G)
+        for t in range(T):
+            tanh(0, t)
+        late_weights()
+        quant_x(1)
+        turn_h(0, 0)
+        turn_h(0, 1)
+        mm1(1, 0)
+        mm1(1, 1, FM)
+        turn_h(0, 2, 1)
+        turn_h(0, 3)
+        mm1(1, 2, FM + 1)
+        load(4)
+        cast(3, 0, S)
+        scale_out(2, 0)
+        turn_x(2, 1)
+        tanh(1, 0)
+        mm1(1, 3)
+        for j in range(TILES):
+            stats(0, j)
+        for j in range(TILES):
+            moments(0, j)
+        late_weights_quantised()
+        add_eps(0)
+        inv_root(0)
+        scale_out(2, 1)
+        tanh(1, 1)
+        late_bias()
+        tanh(1, 2)
+        cast(3, 1, S)
+        load(5)
+        for i in range(3, nch):
+            c_cast, c_scale, c_tanh, c_stat, c_norm, c_late, c_quant = range(i + 1, i - 6, -1)
+            fill = c_quant < 0
+            on(load, i + 3)
+            shift(c_norm)
+            if fill:
+                turn_x(c_scale, 0)
+                tanh(c_stat, 3)
+                normalise(c_norm, 3, S)
+            else:
+                affine(c_late, 3, 0, S)
+                affine(c_late, 3, 1, S)
+                quant_y(c_quant)
+                mm2(c_quant)
+            quant_x(c_tanh)
+            if fill:
+                on(affine, c_late, 3, 0, V)
+                on(affine, c_late, 3, 1, V)
+            on(weave, c_late, 0, N, G)
+            if not fill:
+                tanh(c_stat, 3)
+                normalise(c_norm, 3, S)
+            normalise(c_norm, 0, V)
+            on(finish, c_quant)
+            mm1(c_tanh, 0)
+            if not fill:
+                turn_x(c_scale, 0)
+            on(cast, c_cast, 0, S)
+            normalise(c_norm, 1, V)
+            normalise(c_norm, 2, V)
+            turn_h(c_stat, 3, 1 if fill else 0)
+            turn_z(c_norm, 0, 0)
+            turn_h(c_stat, 0, 0)
+            turn_h(c_stat, 1)
+            tanh(c_tanh, 0)
+            mm1(c_tanh, 1)
+            turn_h(c_stat, 2, 1)
+            on(cast, c_cast, 1, S)
+            scale_out(c_scale, 0)
+            turn_z(c_norm, 1, 0)
+            turn_x(c_scale, 1)
+            affine(c_norm, 0, 0, S)
+            affine(c_norm, 0, 1, S)
+            tanh(c_tanh, 1)
+            mm1(c_tanh, 2)
+            turn_z(c_norm, 2, 1)
+            for j in (3, 0, 1, 2):
+                stats(c_stat, j)
+            for j in (3, 0, 1, 2):
+                moments(c_stat, j)
+            add_eps(c_stat)
+            inv_root(c_stat)
+            scale_out(c_scale, 1)
+            affine(c_norm, 1, 0, S)
+            affine(c_norm, 1, 1, S)
+            turn_z(c_norm, 3, 2)
+            tanh(c_tanh, 2)
+            mm1(c_tanh, 3)
+            affine(c_norm, 2, 0, S)
+            affine(c_norm, 2, 1, S)
 
-        last = nch - 1
-        weave_pool(last - 3)
-        mm2(last - 4)
-        for j in range(SIZES[last]):
-            add_bias(last, j)
-        affine(last - 2, 0)
-        moments(last - 1)
-        inv_root(last - 1)
-        turn_z(last - 2, 3)
-        finish(last - 4)
-        for j in range(SIZES[last]):
-            tanh(last, j)
-        affine(last - 2, 1)
-        for j in range(SIZES[last]):
-            square(last, j)
-        affine(last - 2, 2)
-        moments(last)
-        affine(last - 2, 3)
-        shift(last - 1)
-        for j in range(4):
-            normalise(last - 1, j)
-        inv_root(last)
-        weave_vector(last - 3)
-        shift(last)
-        for j in range(SIZES[last]):
-            normalise(last, j)
-        quant_y(last - 3)
-        for c in (last - 1, last):
-            for t in range(3):
-                turn_z(c, t)
-            affine(c, 0)
-            turn_z(c, 3)
-            mm2(c - 2)
-            for t in range(1, 4):
-                affine(c, t)
-            weave_pool(c - 1)
-            weave_vector(c - 1)
-            finish(c - 2)
-            quant_y(c - 1)
-        weave_scalar(last)
-        mm2(last - 1)
-        quant_y(last)
-        mm2(last)
-        finish(last - 1)
-        finish(last)
+        b, c, d, e, f = range(nch - 5, nch)
+        shift(d)
+        affine(c, 3, 0, S)
+        affine(c, 3, 1, S)
+        quant_y(b)
+        mm2(b)
+        quant_x(f)
+        weave(c, 0, 448, G)
+        tanh(e, 3)
+        mm1(f, 0)
+        normalise(d, 0, V)
+        turn_h(e, 0, 1)
+        normalise(d, 1, V)
+        normalise(d, 3, S)
+        normalise(d, 2, S)
+        finish(b)
+        turn_h(e, 1)
+        turn_h(e, 3)
+        mm1(f, 1, X)
+        turn_h(e, 2)
+        turn_z(d, 0)
+        tanh(f, 0)
+        mm1(f, 2)
+        turn_z(d, 1, 1)
+        tanh(f, 1)
+        mm1(f, 3, X)
+        for j in (0, 1, 3, 2):
+            stats(e, j)
+        affine(d, 0, 0, S)
+        affine(d, 0, 1, S)
+        turn_z(d, 2, 1)
+        for j in (0, 1, 3, 2):
+            moments(e, j)
+        affine(d, 1, 0, V)
+        add_eps(e)
+        inv_root(e)
+        affine(d, 1, 1, V)
+        tanh(f, 2)
+        tanh(f, 3)
+        turn_z(d, 3, 1, S1)
+        affine(d, 2, 0, V)
+
+        shift(e)
+        affine(d, 2, 1, S)
+        normalise(e, 0, V)
+        turn_h(f, 0, 2)
+        weave(c, 448, N, V)
+        normalise(e, 2, S)
+        normalise(e, 3, S)
+        normalise(e, 1, V)
+        turn_h(f, 1, 1)
+        turn_h(f, 2)
+        turn_h(f, 3)
+        quant_y(c)
+        affine(d, 3, 0, S)
+        affine(d, 3, 1, S)
+        weave(d, 0, 256, G)
+        turn_z(e, 0)
+        mm2(c)
+        turn_z(e, 1)
+        turn_z(e, 2, 1, S1)
+        for j in range(TILES):
+            stats(f, j)
+        affine(e, 0, 0, S)
+        affine(e, 0, 1, S)
+        turn_z(e, 3, 1, FM)
+        for j in range(TILES):
+            moments(f, j)
+        finish(c)
+        add_eps(f)
+        inv_root(f)
+        for t in (1, 2):
+            affine(e, t, 0, S)
+            affine(e, t, 1, S)
+        affine(e, 3, 0, V)
+        affine(e, 3, 1, V)
+
+        shift(f)
+        normalise(f, 0, S)
+        normalise(f, 1, S)
+        for t in range(T):
+            turn_z("a", t, 0, (FM + 1, S1, FM, HT)[t])
+        normalise(f, 2, S)
+        normalise(f, 3, S)
+        weave(d, 256, N, V)
+        quant_y(d)
+        mm2(d, X)
+        for t in range(T):
+            affine("a", t, 0, S)
+            affine("a", t, 1, S)
+        for t in range(T):
+            turn_z("b", t, 0, (HT + 1, HT + 2, HT + 3, FM + 1)[t])
+        weave(e, 0, N, V)
+        finish(d)
+        quant_y(e)
+        mm2(e, S1)
+        for t in range(T):
+            affine("b", t, 0, S)
+            affine("b", t, 1, S)
+        weave("b", 0, N // 4, S)
+        weave("a", 0, N // 2, V)
+        finish(e)
+        quant_y("a")
+        mm2("a", FM)
+        weave("b", N // 4, N // 2, V)
+        finish("a")
+        quant_y("b")
+        mm2("b", HT)
+        finish("b")

@@ -365,15 +365,15 @@ def tile_rnnclassifier_pa_t_kernel(tc, h1_bytes, h1_scale, W_ih1, b_ih1, b_hh1, 
             fill = c_quant < 0
             on(load, i + 3)
             shift(c_norm)
+            turn_x(c_scale, 0)
             if fill:
-                turn_x(c_scale, 0)
                 tanh(c_stat, 3)
                 normalise(c_norm, 3, S)
             else:
                 affine(c_late, 3, 0, S)
                 affine(c_late, 3, 1, S)
                 quant_y(c_quant)
-                mm2(c_quant)
+                mm2(c_quant, FM)
             quant_x(c_tanh)
             if fill:
                 on(affine, c_late, 3, 0, V)
@@ -383,32 +383,30 @@ def tile_rnnclassifier_pa_t_kernel(tc, h1_bytes, h1_scale, W_ih1, b_ih1, b_hh1, 
                 tanh(c_stat, 3)
                 normalise(c_norm, 3, S)
             normalise(c_norm, 0, V)
+            normalise(c_norm, 1, V)
             on(finish, c_quant)
             mm1(c_tanh, 0)
-            if not fill:
-                turn_x(c_scale, 0)
             on(cast, c_cast, 0, S)
-            normalise(c_norm, 1, V)
             normalise(c_norm, 2, V)
-            turn_h(c_stat, 3, 1 if fill else 0)
+            turn_h(c_stat, 0, 2)
+            turn_h(c_stat, 3, 0)
+            turn_h(c_stat, 1, 0)
             turn_z(c_norm, 0, 0)
-            turn_h(c_stat, 0, 0)
-            turn_h(c_stat, 1)
             tanh(c_tanh, 0)
             mm1(c_tanh, 1)
             turn_h(c_stat, 2, 1)
             on(cast, c_cast, 1, S)
             scale_out(c_scale, 0)
-            turn_z(c_norm, 1, 0)
+            turn_z(c_norm, 1, 1)
             turn_x(c_scale, 1)
             affine(c_norm, 0, 0, S)
             affine(c_norm, 0, 1, S)
             tanh(c_tanh, 1)
             mm1(c_tanh, 2)
             turn_z(c_norm, 2, 1)
-            for j in (3, 0, 1, 2):
+            for j in (0, 3, 1, 2):
                 stats(c_stat, j)
-            for j in (3, 0, 1, 2):
+            for j in (0, 3, 1, 2):
                 moments(c_stat, j)
             add_eps(c_stat)
             inv_root(c_stat)

@@ -59,9 +59,9 @@ def tile_rnnclassifier_pa_t_kernel(tc, h1_bytes, h1_scale, W_ih1, b_ih1, b_hh1, 
         half = const.tile([P, 4], F32, name="half")
         nc.gpsimd.memset(half[:], -0.5)
 
-        mvs = const.tile([P, nch, 4, 3], F32, name="mvs")
-        nc.gpsimd.memset(mvs[:], 1.0)
-        nc.gpsimd.tensor_scalar(out=mvs[:], in0=mvs[:], scalar1=EPS, scalar2=0.0, op0=ALU.mult, op1=ALU.add)
+        sums = const.tile([P, TILES, 9], F32, name="sums")
+        nc.gpsimd.memset(sums[:], 0.0)
+        nc.gpsimd.tensor_scalar(out=sums[:, :, 8], in0=sums[:, :, 8], scalar1=0.0, scalar2=EPS * H, op0=ALU.mult, op1=ALU.add)
 
         w_sb = {}
 
@@ -169,22 +169,16 @@ def tile_rnnclassifier_pa_t_kernel(tc, h1_bytes, h1_scale, W_ih1, b_ih1, b_hh1, 
                 turn(ht[c, j][:, t * P : (t + 1) * P], hh[c, t][:, j * P : (j + 1) * P], t < plain)
 
         def stats(c, j):
-            bn[c, j] = stat.tile([P, 6], F32, name="bn", bufs=4)
-            nc.vector.bn_stats(out=bn[c, j][:], in_=ht[c, j][:])
+            nc.vector.bn_stats(out=sums[:, j, 0:6], in_=ht[c, j][:])
 
         def moments(c, j):
             if c not in mv:
-                mv[c] = mvs[:, c]
-            nc.vector.bn_aggr(out=mv[c][:, j, 0:2], in_=bn[c, j][:])
-
-        def add_eps(c):
-            n = SIZES[c]
-            rs[c] = stat.tile([P, 4], F32, name="rs")
-            nc.vector.tensor_reduce(out=rs[c][:, :n], in_=mv[c][:, :n, 1:3], axis=mybir.AxisListType.X, op=ALU.add)
+                mv[c] = stat.tile([P, TILES, 2], F32, name="mv")
+            nc.vector.bn_aggr(out=mv[c][:, j, :], in_=sums[:, j, :])
 
         def inv_root(c):
-            n = SIZES[c]
-            nc.gpsimd.tensor_tensor(out=rs[c][:, :n], in0=rs[c][:, :n], in1=half[:, :n], op=ALU.pow)
+            rs[c] = stat.tile([P, TILES], F32, name="rs")
+            nc.gpsimd.tensor_tensor(out=rs[c][:], in0=mv[c][:, :, 1], in1=half[:], op=ALU.pow)
 
         def shift(c):
             n = SIZES[c]
@@ -352,7 +346,6 @@ def tile_rnnclassifier_pa_t_kernel(tc, h1_bytes, h1_scale, W_ih1, b_ih1, b_hh1, 
         for j in range(TILES):
             moments(0, j)
         late_weights_quantised()
-        add_eps(0)
         inv_root(0)
         scale_out(2, 1)
         tanh(1, 1)
@@ -408,7 +401,6 @@ def tile_rnnclassifier_pa_t_kernel(tc, h1_bytes, h1_scale, W_ih1, b_ih1, b_hh1, 
                 stats(c_stat, j)
             for j in (0, 3, 1, 2):
                 moments(c_stat, j)
-            add_eps(c_stat)
             inv_root(c_stat)
             scale_out(c_scale, 1)
             affine(c_norm, 1, 0, S)
@@ -453,7 +445,6 @@ def tile_rnnclassifier_pa_t_kernel(tc, h1_bytes, h1_scale, W_ih1, b_ih1, b_hh1, 
         for j in (0, 1, 3, 2):
             moments(e, j)
         affine(d, 1, 0, V)
-        add_eps(e)
         inv_root(e)
         affine(d, 1, 1, V)
         tanh(f, 2)
@@ -488,7 +479,6 @@ def tile_rnnclassifier_pa_t_kernel(tc, h1_bytes, h1_scale, W_ih1, b_ih1, b_hh1, 
         for j in range(TILES):
             moments(f, j)
         finish(c)
-        add_eps(f)
         inv_root(f)
         for t in (1, 2):
             affine(e, t, 0, S)

@@ -22,8 +22,8 @@ HH_BUFS = 8
 X, S1, FM, HT = 0, 1, 2, 4
 TILES = 4
 PARTS = {"a": (15, 0, 2), "b": (15, 2, 2)}
-HX_BUFS = 6
-XB_BUFS = 5
+HX_BUFS = 8
+XB_BUFS = 6
 
 
 def tile_rnnclassifier_pa_t_kernel(tc, h1_bytes, h1_scale, W_ih1, b_ih1, b_hh1, ln_g, ln_b, fc_W, fc_b, out):
@@ -106,8 +106,11 @@ def tile_rnnclassifier_pa_t_kernel(tc, h1_bytes, h1_scale, W_ih1, b_ih1, b_hh1, 
         def words(ap):
             return ap.bitcast(F32)
 
-        def cast(c, h, eng):
-            hx[c, h] = work.tile([P, 2 * H], BF16, name="hx", align_bytes=64, bufs=HX_BUFS)
+        def cast(c, h, eng, after=None):
+            if after is None:
+                hx[c, h] = work.tile([P, 2 * H], BF16, name="hx", align_bytes=64, bufs=HX_BUFS)
+            else:
+                hx[c, h] = work.tile([P, 2 * H], BF16, name="xg%d" % (after % 3), align_bytes=64, bufs=1)
             if eng is nc.scalar:
                 nc.scalar.copy(out=hx[c, h][:], in_=xb[c, h].bitcast(FP8))
             else:
@@ -126,7 +129,7 @@ def tile_rnnclassifier_pa_t_kernel(tc, h1_bytes, h1_scale, W_ih1, b_ih1, b_hh1, 
 
         def scale_out(c, h):
             if c not in xg:
-                xg[c] = work.tile([P, SIZES[c] * P, T], BF16, name="xg", align_bytes=64)
+                xg[c] = work.tile([P, SIZES[c] * P, T], BF16, name="xg%d" % (c % 3), align_bytes=64, bufs=1)
             n = min(2, SIZES[c] - 2 * h) * P
             nc.vector.tensor_tensor(
                 out=xg[c][:, h * 2 * P : h * 2 * P + n, :].rearrange("p n (u e) -> p n u e", e=2),
@@ -185,13 +188,14 @@ def tile_rnnclassifier_pa_t_kernel(tc, h1_bytes, h1_scale, W_ih1, b_ih1, b_hh1, 
             nm[c] = stat.tile([P, 4], F32, name="nm")
             nc.vector.scalar_tensor_tensor(out=nm[c][:, :n], in0=mv[c][:, :n, 0], scalar=-1.0, in1=rs[c][:, :n], op0=ALU.mult, op1=ALU.mult)
 
-        def normalise(c, j, eng):
-            zz[c, j] = work.tile([P, H], F32, name="zz", bufs=8)
+        def normalise(c, j, eng, lo=0, hi=H):
+            if (c, j) not in zz:
+                zz[c, j] = work.tile([P, H], F32, name="zz", bufs=8)
             rstd = rs[c][:, j : j + 1]
             if eng is nc.vector:
-                nc.vector.tensor_scalar(out=zz[c, j][:], in0=ht[c, j][:], scalar1=mv[c][:, j, 0:1], scalar2=rstd, op0=ALU.subtract, op1=ALU.mult)
+                nc.vector.tensor_scalar(out=zz[c, j][:, lo:hi], in0=ht[c, j][:, lo:hi], scalar1=mv[c][:, j, 0:1], scalar2=rstd, op0=ALU.subtract, op1=ALU.mult)
             else:
-                nc.scalar.activation(out=zz[c, j][:], in_=ht[c, j][:], func=ACT.Identity, scale=rstd, bias=nm[c][:, j : j + 1])
+                nc.scalar.activation(out=zz[c, j][:, lo:hi], in_=ht[c, j][:, lo:hi], func=ACT.Identity, scale=rstd, bias=nm[c][:, j : j + 1])
 
         def tiles(u):
             return PARTS.get(u, (u, 0, TILES))
@@ -213,7 +217,7 @@ def tile_rnnclassifier_pa_t_kernel(tc, h1_bytes, h1_scale, W_ih1, b_ih1, b_hh1, 
 
         def weave(u, lo, hi, eng):
             if u not in yg:
-                yg[u] = work.tile([P, 2, tiles(u)[2] * P, T], BF16, name="yg_end" if u in PARTS else "yg", align_bytes=64, bufs=2 if u in PARTS else 1)
+                yg[u] = work.tile([P, 2, tiles(u)[2] * P, T], BF16, name="yg_%s" % u if u in PARTS or u == nch - 2 else "yg", align_bytes=64, bufs=1)
             dst, src = yg[u][:, :, lo:hi, :], yy[u][:, :, :, lo:hi]
             if eng is nc.gpsimd:
                 nc.gpsimd.tensor_scalar(out=dst, in0=src.rearrange("p o t n -> p o n t"), scalar1=1.0, scalar2=0.0, op0=ALU.mult, op1=ALU.add)
@@ -302,9 +306,9 @@ def tile_rnnclassifier_pa_t_kernel(tc, h1_bytes, h1_scale, W_ih1, b_ih1, b_hh1, 
         N = TILES * P
         cast(0, 0, V)
         turn_x(0, 0)
-        cast(0, 1, V)
-        first_weights(0)
+        cast(0, 1, S)
         turn_x(0, 1, HT)
+        first_weights(0)
         cast(1, 1, S)
         first_weights(1)
         first_bias()
@@ -328,6 +332,11 @@ def tile_rnnclassifier_pa_t_kernel(tc, h1_bytes, h1_scale, W_ih1, b_ih1, b_hh1, 
             tanh(0, t)
         late_weights()
         quant_x(1)
+        load(4)
+        load(5)
+        cast(3, 0, G, 1)
+        cast(3, 1, G)
+        cast(4, 0, G)
         turn_h(0, 0)
         turn_h(0, 1)
         mm1(1, 0)
@@ -335,8 +344,6 @@ def tile_rnnclassifier_pa_t_kernel(tc, h1_bytes, h1_scale, W_ih1, b_ih1, b_hh1, 
         turn_h(0, 2, 1)
         turn_h(0, 3)
         mm1(1, 2, FM + 1)
-        load(4)
-        cast(3, 0, S)
         scale_out(2, 0)
         turn_x(2, 1)
         tanh(1, 0)
@@ -345,50 +352,64 @@ def tile_rnnclassifier_pa_t_kernel(tc, h1_bytes, h1_scale, W_ih1, b_ih1, b_hh1, 
             stats(0, j)
         for j in range(TILES):
             moments(0, j)
-        late_weights_quantised()
         inv_root(0)
         scale_out(2, 1)
         tanh(1, 1)
         late_bias()
         tanh(1, 2)
-        cast(3, 1, S)
-        load(5)
         for i in range(3, nch):
             c_cast, c_scale, c_tanh, c_stat, c_norm, c_late, c_quant = range(i + 1, i - 6, -1)
             fill = c_quant < 0
             on(load, i + 3)
-            shift(c_norm)
+            if fill:
+                shift(c_norm)
             turn_x(c_scale, 0)
             if fill:
-                tanh(c_stat, 3)
+                if c_late < 0:
+                    tanh(c_stat, 3)
                 normalise(c_norm, 3, S)
+                quant_x(c_tanh)
+                on(affine, c_late, 3, 0, V)
+                on(affine, c_late, 3, 1, V)
+                normalise(c_norm, 2, S)
             else:
                 affine(c_late, 3, 0, S)
                 affine(c_late, 3, 1, S)
                 quant_y(c_quant)
                 mm2(c_quant, FM)
-            quant_x(c_tanh)
-            if fill:
-                on(affine, c_late, 3, 0, V)
-                on(affine, c_late, 3, 1, V)
+                shift(c_norm)
+                quant_x(c_tanh)
+            if c_late < 0:
+                late_weights_quantised()
+                cast(c_cast, 1, G, c_tanh)
+                cast(c_cast + 1, 0, G)
+                cast(c_cast + 1, 1, G)
             on(weave, c_late, 0, N, G)
             if not fill:
                 tanh(c_stat, 3)
                 normalise(c_norm, 3, S)
+                normalise(c_norm, 2, S, 384, H)
             normalise(c_norm, 0, V)
             normalise(c_norm, 1, V)
             on(finish, c_quant)
             mm1(c_tanh, 0)
-            on(cast, c_cast, 0, S)
-            normalise(c_norm, 2, V)
-            turn_h(c_stat, 0, 2)
-            turn_h(c_stat, 3, 0)
-            turn_h(c_stat, 1, 0)
-            turn_z(c_norm, 0, 0)
+            if not fill:
+                on(cast, c_cast, 0, S)
+            if not fill:
+                normalise(c_norm, 2, V, 0, 384)
+            order = (3, 2, 0, 1) if fill else (0, 3, 1, 2)
+            turn_h(c_stat, order[0], 1 if fill else 2)
+            turn_h(c_stat, order[1], 0)
+            if fill:
+                turn_z(c_norm, 0, 0)
+            turn_h(c_stat, order[2], 0)
+            if not fill:
+                turn_z(c_norm, 0, 0)
             tanh(c_tanh, 0)
             mm1(c_tanh, 1)
-            turn_h(c_stat, 2, 1)
-            on(cast, c_cast, 1, S)
+            turn_h(c_stat, order[3], 1)
+            if not fill:
+                on(cast, c_cast, 1, S)
             scale_out(c_scale, 0)
             turn_z(c_norm, 1, 1)
             turn_x(c_scale, 1)
@@ -397,9 +418,9 @@ def tile_rnnclassifier_pa_t_kernel(tc, h1_bytes, h1_scale, W_ih1, b_ih1, b_hh1, 
             tanh(c_tanh, 1)
             mm1(c_tanh, 2)
             turn_z(c_norm, 2, 1)
-            for j in (0, 3, 1, 2):
+            for j in order:
                 stats(c_stat, j)
-            for j in (0, 3, 1, 2):
+            for j in order:
                 moments(c_stat, j)
             inv_root(c_stat)
             scale_out(c_scale, 1)
@@ -410,26 +431,28 @@ def tile_rnnclassifier_pa_t_kernel(tc, h1_bytes, h1_scale, W_ih1, b_ih1, b_hh1, 
             mm1(c_tanh, 3)
             affine(c_norm, 2, 0, S)
             affine(c_norm, 2, 1, S)
+            if c_late < 0:
+                tanh(c_tanh, 3)
 
         b, c, d, e, f = range(nch - 5, nch)
-        shift(d)
         affine(c, 3, 0, S)
         affine(c, 3, 1, S)
         quant_y(b)
         mm2(b)
+        shift(d)
         quant_x(f)
-        weave(c, 0, 448, G)
+        weave(c, 0, 416, G)
         tanh(e, 3)
-        mm1(f, 0)
         normalise(d, 0, V)
-        turn_h(e, 0, 1)
         normalise(d, 1, V)
+        turn_h(e, 0)
+        mm1(f, 0)
+        turn_h(e, 1)
+        finish(b)
         normalise(d, 3, S)
         normalise(d, 2, S)
-        finish(b)
-        turn_h(e, 1)
-        turn_h(e, 3)
         mm1(f, 1, X)
+        turn_h(e, 3)
         turn_h(e, 2)
         turn_z(d, 0)
         tanh(f, 0)
@@ -442,79 +465,78 @@ def tile_rnnclassifier_pa_t_kernel(tc, h1_bytes, h1_scale, W_ih1, b_ih1, b_hh1, 
         affine(d, 0, 0, S)
         affine(d, 0, 1, S)
         turn_z(d, 2, 1)
-        for j in (0, 1, 3, 2):
-            moments(e, j)
-        affine(d, 1, 0, V)
-        inv_root(e)
-        affine(d, 1, 1, V)
         tanh(f, 2)
         tanh(f, 3)
-        turn_z(d, 3, 1, S1)
-        affine(d, 2, 0, V)
+        for j in (0, 1, 3, 2):
+            moments(e, j)
+        inv_root(e)
+        affine(d, 1, 0, V)
+        affine(d, 1, 1, V)
+        turn_z(d, 3, 2)
+        affine(d, 2, 0, S)
+        affine(d, 2, 1, S)
 
         shift(e)
-        affine(d, 2, 1, S)
         normalise(e, 0, V)
         turn_h(f, 0, 2)
-        weave(c, 448, N, V)
+        weave(c, 416, N, V)
         normalise(e, 2, S)
         normalise(e, 3, S)
         normalise(e, 1, V)
-        turn_h(f, 1, 1)
-        turn_h(f, 2)
-        turn_h(f, 3)
+        turn_h(f, 2, 0)
+        turn_z(e, 0)
+        turn_h(f, 1)
         quant_y(c)
         affine(d, 3, 0, S)
         affine(d, 3, 1, S)
         weave(d, 0, 256, G)
-        turn_z(e, 0)
-        mm2(c)
+        turn_h(f, 3, 1)
         turn_z(e, 1)
+        mm2(c)
         turn_z(e, 2, 1, S1)
-        for j in range(TILES):
+        for j in (0, 2, 1, 3):
             stats(f, j)
         affine(e, 0, 0, S)
         affine(e, 0, 1, S)
         turn_z(e, 3, 1, FM)
-        for j in range(TILES):
+        for j in (0, 2, 1, 3):
             moments(f, j)
-        finish(c)
         inv_root(f)
+        finish(c)
+        affine(e, 3, 0, V)
         for t in (1, 2):
             affine(e, t, 0, S)
             affine(e, t, 1, S)
-        affine(e, 3, 0, V)
         affine(e, 3, 1, V)
 
-        shift(f)
-        normalise(f, 0, S)
-        normalise(f, 1, S)
+        weave(d, 256, N, G)
+        weave(e, 0, 256, S)
+        normalise(f, 0, V)
+        normalise(f, 1, V)
         for t in range(T):
-            turn_z("a", t, 0, (FM + 1, S1, FM, HT)[t])
-        normalise(f, 2, S)
-        normalise(f, 3, S)
-        weave(d, 256, N, V)
+            turn_z("a", t, 0, (X, HT, HT + 1, FM + 1)[t])
+        normalise(f, 2, V)
+        normalise(f, 3, V)
+        for t in range(T):
+            turn_z("b", t, 0, (S1, HT + 2, HT + 3, FM)[t])
         quant_y(d)
-        mm2(d, X)
         for t in range(T):
             affine("a", t, 0, S)
             affine("a", t, 1, S)
-        for t in range(T):
-            turn_z("b", t, 0, (HT + 1, HT + 2, HT + 3, FM + 1)[t])
-        weave(e, 0, N, V)
-        finish(d)
+        mm2(d, X)
+        weave(e, 256, N, V)
         quant_y(e)
-        mm2(e, S1)
+        mm2(e, HT)
+        finish(d)
         for t in range(T):
             affine("b", t, 0, S)
             affine("b", t, 1, S)
-        weave("b", 0, N // 4, S)
+        weave("b", 0, N // 2, S)
         weave("a", 0, N // 2, V)
         finish(e)
         quant_y("a")
-        mm2("a", FM)
-        weave("b", N // 4, N // 2, V)
-        finish("a")
+        mm2("a", HT + 1)
         quant_y("b")
-        mm2("b", HT)
+        mm2("b", FM + 1)
+        finish("a")
         finish("b")

@@ -6,6 +6,9 @@ from concourse.masks import make_identity
 B, H, H2, D_OUT = 8192, 512, 1024, 128
 P = 128
 T = 4
+TILES = 4
+N = TILES * P
+CHUNKS = B // N
 EPS = 1e-5
 FLOPS = 2 * B * H * H + 2 * B * H2 * D_OUT
 
@@ -17,23 +20,21 @@ FP8 = mybir.dt.float8_e4m3fn
 FP8X4 = mybir.dt.float8_e4m3fn_x4
 ACT = mybir.ActivationFunctionType
 ALU = mybir.AluOpType
-SIZES = [4] * 16
-HH_BUFS = 8
-X, S1, FM, HT = 0, 1, 2, 4
-TILES = 4
-PARTS = {"a": (15, 0, 2), "b": (15, 2, 2)}
-HX_BUFS = 8
-XB_BUFS = 6
+
+WORDS, FIRST, PLANES, HELD = 0, 1, 2, 4
+
+HALVES = {"a": (CHUNKS - 1, 0, 2), "b": (CHUNKS - 1, 2, 2)}
+
+NORMALISE_ON_VECTOR = 256
+WEAVE_SHORT = 416
 
 
 def tile_rnnclassifier_pa_t_kernel(tc, h1_bytes, h1_scale, W_ih1, b_ih1, b_hh1, ln_g, ln_b, fc_W, fc_b, out):
     nc = tc.nc
-    first = [sum(SIZES[:c]) * P for c in range(len(SIZES))]
-    nch = len(SIZES)
+    V, S, G = nc.vector, nc.scalar, nc.gpsimd
 
     def rows(ap, c):
-        n = SIZES[c]
-        return ap[first[c] : first[c] + n * P, :].rearrange("(q j) k -> q j k", j=n)
+        return ap[c * N : (c + 1) * N, :].rearrange("(q j) k -> q j k", j=TILES)
 
     with ExitStack() as ctx:
         const = ctx.enter_context(tc.tile_pool(name="const", bufs=1))
@@ -43,20 +44,20 @@ def tile_rnnclassifier_pa_t_kernel(tc, h1_bytes, h1_scale, W_ih1, b_ih1, b_hh1, 
         ctx.enter_context(tc.manual_schedule())
 
         xb, hx, xg, xc, xs = {}, {}, {}, {}, {}
-        hh, ht, zz, bn, mv, rs, nm = {}, {}, {}, {}, {}, {}, {}
+        hh, ht, zz, mv, rs, nm = {}, {}, {}, {}, {}, {}
         yy, yg, yc, ys = {}, {}, {}, {}
-        osb, fmb, xtb, s1b, ob = {}, {}, {}, {}, {}
+        fmb, xtb, s1b, ob = {}, {}, {}, {}
 
         def load(c, h=None):
             j0, m = (0, TILES) if h is None else (2 * h, 2)
-            raw = work.tile([P, m * H], U8, name="x_bytes", align_bytes=64, bufs=XB_BUFS)
+            raw = work.tile([P, m * H], U8, name="x_bytes", align_bytes=64, bufs=6)
             nc.sync.dma_start(out=raw[:].rearrange("p (j k) -> p j k", k=H), in_=rows(h1_bytes, c)[:, j0 : j0 + m, :])
             for g in range(m // 2):
                 xb[c, j0 // 2 + g] = raw[:, 2 * g * H : 2 * (g + 1) * H]
 
         ident = const.tile([P, P], F32, name="ident")
         make_identity(nc, ident[:])
-        half = const.tile([P, 4], F32, name="half")
+        half = const.tile([P, TILES], F32, name="half")
         nc.gpsimd.memset(half[:], -0.5)
 
         sums = const.tile([P, TILES, 9], F32, name="sums")
@@ -108,10 +109,10 @@ def tile_rnnclassifier_pa_t_kernel(tc, h1_bytes, h1_scale, W_ih1, b_ih1, b_hh1, 
 
         def cast(c, h, eng, after=None):
             if after is None:
-                hx[c, h] = work.tile([P, 2 * H], BF16, name="hx", align_bytes=64, bufs=HX_BUFS)
+                hx[c, h] = work.tile([P, 2 * H], BF16, name="hx", align_bytes=64, bufs=8)
             else:
                 hx[c, h] = work.tile([P, 2 * H], BF16, name="xg%d" % (after % 3), align_bytes=64, bufs=1)
-            if eng is nc.scalar:
+            if eng is S:
                 nc.scalar.copy(out=hx[c, h][:], in_=xb[c, h].bitcast(FP8))
             else:
                 eng.tensor_copy(out=hx[c, h][:], in_=xb[c, h].bitcast(FP8))
@@ -119,33 +120,31 @@ def tile_rnnclassifier_pa_t_kernel(tc, h1_bytes, h1_scale, W_ih1, b_ih1, b_hh1, 
         def bank(k, shape):
             return psum.tile(shape, F32, name="bank%d" % k)
 
-        def turn_x(c, h, kind=X):
-            m = min(2, SIZES[c] - 2 * h)
-            xtb[c, h] = bank(kind, [P, 2, m * P])
-            for jj in range(m):
+        def turn_x(c, h, k=WORDS):
+            xtb[c, h] = bank(k, [P, 2, 2 * P])
+            for jj in range(2):
                 w = words(hx[c, h][:, jj * H : (jj + 1) * H])
                 for u in range(2):
                     nc.tensor.transpose(xtb[c, h][:, u, jj * P : (jj + 1) * P], w[:, u : H // 2 : 2], ident[:])
 
         def scale_out(c, h):
             if c not in xg:
-                xg[c] = work.tile([P, SIZES[c] * P, T], BF16, name="xg%d" % (c % 3), align_bytes=64, bufs=1)
-            n = min(2, SIZES[c] - 2 * h) * P
+                xg[c] = work.tile([P, N, T], BF16, name="xg%d" % (c % 3), align_bytes=64, bufs=1)
+            n = 2 * P
             nc.vector.tensor_tensor(
-                out=xg[c][:, h * 2 * P : h * 2 * P + n, :].rearrange("p n (u e) -> p n u e", e=2),
+                out=xg[c][:, h * n : (h + 1) * n, :].rearrange("p n (u e) -> p n u e", e=2),
                 in0=xtb[c, h][:].bitcast(BF16).rearrange("p u (n e) -> p n u e", e=2),
                 in1=s4[:].rearrange("p (u e) -> p u e", e=2).unsqueeze(1).to_broadcast([P, n, 2, 2]),
                 op=ALU.mult,
             )
 
         def quant_x(c):
-            n = SIZES[c] * P
-            xc[c] = work.tile([P, n], U32, name="xc", align_bytes=64)
-            xs[c] = work.tile([P, n], U8, name="xs", align_bytes=64)
+            xc[c] = work.tile([P, N], U32, name="xc", align_bytes=64)
+            xs[c] = work.tile([P, N], U8, name="xs", align_bytes=64)
             nc.vector.quantize_mx(out=xc[c][:].bitcast(FP8X4), scales=xs[c][:], in_=xg[c][:].rearrange("p n t -> p (n t)"))
 
-        def mm1(c, t, kind=S1):
-            s1b[c, t] = bank(kind, [P, SIZES[c] * P])
+        def mm1(c, t, k=FIRST):
+            s1b[c, t] = bank(k, [P, N])
             nc.tensor.matmul_mx(
                 out=s1b[c, t][:],
                 lhsT=w_codes[:, t * P : (t + 1) * P].bitcast(FP8X4),
@@ -157,7 +156,7 @@ def tile_rnnclassifier_pa_t_kernel(tc, h1_bytes, h1_scale, W_ih1, b_ih1, b_hh1, 
             )
 
         def tanh(c, t):
-            hh[c, t] = work.tile([P, SIZES[c] * P], F32, name="hh", bufs=HH_BUFS)
+            hh[c, t] = work.tile([P, N], F32, name="hh", bufs=2 * T)
             nc.scalar.activation(out=hh[c, t][:], in_=s1b[c, t][:], func=ACT.Tanh, bias=bias[:, t : t + 1])
 
         def turn(dst, src, plain):
@@ -166,8 +165,8 @@ def tile_rnnclassifier_pa_t_kernel(tc, h1_bytes, h1_scale, W_ih1, b_ih1, b_hh1, 
             else:
                 nc.tensor.transpose(dst, src, ident[:])
 
-        def turn_h(c, j, plain=0, kind=None):
-            ht[c, j] = bank(HT + j if kind is None else kind, [P, H])
+        def turn_h(c, j, plain=0):
+            ht[c, j] = bank(HELD + j, [P, H])
             for t in range(T):
                 turn(ht[c, j][:, t * P : (t + 1) * P], hh[c, t][:, j * P : (j + 1) * P], t < plain)
 
@@ -184,25 +183,24 @@ def tile_rnnclassifier_pa_t_kernel(tc, h1_bytes, h1_scale, W_ih1, b_ih1, b_hh1, 
             nc.gpsimd.tensor_tensor(out=rs[c][:], in0=mv[c][:, :, 1], in1=half[:], op=ALU.pow)
 
         def shift(c):
-            n = SIZES[c]
-            nm[c] = stat.tile([P, 4], F32, name="nm")
-            nc.vector.scalar_tensor_tensor(out=nm[c][:, :n], in0=mv[c][:, :n, 0], scalar=-1.0, in1=rs[c][:, :n], op0=ALU.mult, op1=ALU.mult)
+            nm[c] = stat.tile([P, TILES], F32, name="nm")
+            nc.vector.scalar_tensor_tensor(out=nm[c][:], in0=mv[c][:, :, 0], scalar=-1.0, in1=rs[c][:], op0=ALU.mult, op1=ALU.mult)
 
         def normalise(c, j, eng, lo=0, hi=H):
             if (c, j) not in zz:
-                zz[c, j] = work.tile([P, H], F32, name="zz", bufs=8)
+                zz[c, j] = work.tile([P, H], F32, name="zz", bufs=2 * TILES)
             rstd = rs[c][:, j : j + 1]
-            if eng is nc.vector:
+            if eng is V:
                 nc.vector.tensor_scalar(out=zz[c, j][:, lo:hi], in0=ht[c, j][:, lo:hi], scalar1=mv[c][:, j, 0:1], scalar2=rstd, op0=ALU.subtract, op1=ALU.mult)
             else:
                 nc.scalar.activation(out=zz[c, j][:, lo:hi], in_=ht[c, j][:, lo:hi], func=ACT.Identity, scale=rstd, bias=nm[c][:, j : j + 1])
 
         def tiles(u):
-            return PARTS.get(u, (u, 0, TILES))
+            return HALVES.get(u, (u, 0, TILES))
 
-        def turn_z(u, t, plain=0, kind=None):
+        def turn_z(u, t, plain=0, k=None):
             c, j0, m = tiles(u)
-            fmb[u, t] = bank(FM + t % 2 if kind is None else kind, [P, m * P])
+            fmb[u, t] = bank(PLANES + t % 2 if k is None else k, [P, m * P])
             for j in range(m):
                 turn(fmb[u, t][:, j * P : (j + 1) * P], zz[c, j0 + j][:, t * P : (t + 1) * P], j < plain)
 
@@ -210,18 +208,19 @@ def tile_rnnclassifier_pa_t_kernel(tc, h1_bytes, h1_scale, W_ih1, b_ih1, b_hh1, 
             if u not in yy:
                 yy[u] = work.tile([P, 2, T, tiles(u)[2] * P], BF16, name="yy", bufs=3)
             gain, offset = g_col[:, o, t : t + 1], b_col[:, o, t : t + 1]
-            if eng is nc.vector:
+            if eng is V:
                 nc.vector.tensor_scalar(out=yy[u][:, o, t, :], in0=fmb[u, t][:], scalar1=gain, scalar2=offset, op0=ALU.mult, op1=ALU.add)
             else:
                 nc.scalar.activation(out=yy[u][:, o, t, :], in_=fmb[u, t][:], func=ACT.Identity, scale=gain, bias=offset)
 
         def weave(u, lo, hi, eng):
             if u not in yg:
-                yg[u] = work.tile([P, 2, tiles(u)[2] * P, T], BF16, name="yg_%s" % u if u in PARTS or u == nch - 2 else "yg", align_bytes=64, bufs=1)
+                tag = "yg_%s" % u if u in HALVES or u == CHUNKS - 2 else "yg"
+                yg[u] = work.tile([P, 2, tiles(u)[2] * P, T], BF16, name=tag, align_bytes=64, bufs=1)
             dst, src = yg[u][:, :, lo:hi, :], yy[u][:, :, :, lo:hi]
-            if eng is nc.gpsimd:
+            if eng is G:
                 nc.gpsimd.tensor_scalar(out=dst, in0=src.rearrange("p o t n -> p o n t"), scalar1=1.0, scalar2=0.0, op0=ALU.mult, op1=ALU.add)
-            elif eng is nc.vector:
+            elif eng is V:
                 nc.vector.tensor_copy(out=dst.rearrange("p o (n i) t -> p o n t i", i=4), in_=src.rearrange("p o t (n i) -> p o n t i", i=4))
             else:
                 for o in range(2):
@@ -233,9 +232,9 @@ def tile_rnnclassifier_pa_t_kernel(tc, h1_bytes, h1_scale, W_ih1, b_ih1, b_hh1, 
             ys[u] = work.tile([P, 2 * n], U8, name="ys", align_bytes=64)
             nc.vector.quantize_mx(out=yc[u][:].bitcast(FP8X4), scales=ys[u][:], in_=yg[u][:].rearrange("p o n t -> p (o n t)"))
 
-        def mm2(u, kind=X):
+        def mm2(u, k=WORDS):
             m = tiles(u)[2]
-            ob[u] = bank(kind, [P, m, D_OUT])
+            ob[u] = bank(k, [P, m, D_OUT])
             for j in range(m):
                 for o in range(2):
                     cols = slice((o * m + j) * P, (o * m + j + 1) * P)
@@ -251,12 +250,12 @@ def tile_rnnclassifier_pa_t_kernel(tc, h1_bytes, h1_scale, W_ih1, b_ih1, b_hh1, 
 
         def finish(u):
             c, j0, m = tiles(u)
-            osb[u] = work.tile([P, m, D_OUT], F32, name="osb", bufs=3)
-            nc.vector.tensor_tensor(out=osb[u][:], in0=ob[u][:], in1=fcb[:].unsqueeze(1).to_broadcast([P, m, D_OUT]), op=ALU.add)
-            nc.sync.dma_start(out=rows(out, c)[:, j0 : j0 + m, :], in_=osb[u][:])
+            osb = work.tile([P, m, D_OUT], F32, name="osb", bufs=3)
+            nc.vector.tensor_tensor(out=osb[:], in0=ob[u][:], in1=fcb[:].unsqueeze(1).to_broadcast([P, m, D_OUT]), op=ALU.add)
+            nc.sync.dma_start(out=rows(out, c)[:, j0 : j0 + m, :], in_=osb[:])
 
-        def turn_weights(pieces, grp, kind):
-            xt = bank(kind, [P, 4 * P])
+        def turn_weights(pieces, grp, k):
+            xt = bank(k, [P, 4 * P])
             v = xt[:].rearrange("p (a u r) -> p a u r", a=2, u=2)
             for a in range(2):
                 for u in range(2):
@@ -264,7 +263,7 @@ def tile_rnnclassifier_pa_t_kernel(tc, h1_bytes, h1_scale, W_ih1, b_ih1, b_hh1, 
             nc.scalar.copy(out=words(grp).rearrange("p (j r) u -> p j r u", j=2), in_=v.rearrange("p j u r -> p j r u"))
 
         def first_weights(h):
-            turn_weights([words(w_sb[h][:, a, :]) for a in range(2)], w_grp[:, h * 256 : h * 256 + 256, :], FM + h)
+            turn_weights([words(w_sb[h][:, a, :]) for a in range(2)], w_grp[:, h * 2 * P : (h + 1) * 2 * P, :], PLANES + h)
 
         def first_bias():
             nc.gpsimd.tensor_tensor(out=bias[:], in0=bi_raw[:], in1=bh_raw[:], op=ALU.add)
@@ -279,35 +278,32 @@ def tile_rnnclassifier_pa_t_kernel(tc, h1_bytes, h1_scale, W_ih1, b_ih1, b_hh1, 
             nc.gpsimd.tensor_copy(out=fb_col[:], in_=fb_raw[:])
 
         def late_bias():
-            fk = bank(FM, [P, D_OUT])
+            fk = bank(PLANES, [P, D_OUT])
             nc.tensor.transpose(fk[:], fb_col[:].to_broadcast([P, P]), ident[:])
             nc.scalar.copy(out=fcb[:], in_=fk[:])
 
         def late_weights():
             fw = words(f_sb[:])
-            turn_weights([fw[:, 256 * o : 256 * (o + 1)] for o in range(2)], f_grp[:], HT + 2)
+            turn_weights([fw[:, o * H // 2 : (o + 1) * H // 2] for o in range(2)], f_grp[:], HELD + 2)
 
         def late_weights_quantised():
             nc.vector.quantize_mx(out=f_codes[:].bitcast(FP8X4), scales=f_scales[:], in_=f_grp[:].rearrange("p n t -> p (n t)"))
 
-        def on(fn, c, *args):
-            if 0 <= c < nch:
-                fn(c, *args)
+        def affines(u, t, eng):
+            for o in range(2):
+                affine(u, t, o, eng)
 
-        def on_tile(fn, c, j, *args):
-            if 0 <= c < nch and j < SIZES[c]:
-                fn(c, j, *args)
+        def statistics(c, order):
+            for j in order:
+                stats(c, j)
+            for j in order:
+                moments(c, j)
+            inv_root(c)
 
-        def on_pair(fn, c, h, *args):
-            if 0 <= c < nch and 2 * h < SIZES[c]:
-                fn(c, h, *args)
-
-        V, S, G = nc.vector, nc.scalar, nc.gpsimd
-        N = TILES * P
         cast(0, 0, V)
         turn_x(0, 0)
         cast(0, 1, S)
-        turn_x(0, 1, HT)
+        turn_x(0, 1, HELD)
         first_weights(0)
         cast(1, 1, S)
         first_weights(1)
@@ -316,12 +312,12 @@ def tile_rnnclassifier_pa_t_kernel(tc, h1_bytes, h1_scale, W_ih1, b_ih1, b_hh1, 
         scale_out(0, 0)
         scale_out(0, 1)
         turn_x(1, 0)
-        turn_x(1, 1, HT + 1)
+        turn_x(1, 1, HELD + 1)
         first_weights_quantised(0)
         quant_x(0)
         first_weights_quantised(1)
-        for t, kind in enumerate((S1, FM, FM + 1, HT + 3)):
-            mm1(0, t, kind)
+        for t, k in enumerate((FIRST, PLANES, PLANES + 1, HELD + 3)):
+            mm1(0, t, k)
         cast(2, 0, S)
         scale_out(1, 0)
         turn_x(2, 0)
@@ -340,108 +336,112 @@ def tile_rnnclassifier_pa_t_kernel(tc, h1_bytes, h1_scale, W_ih1, b_ih1, b_hh1, 
         turn_h(0, 0)
         turn_h(0, 1)
         mm1(1, 0)
-        mm1(1, 1, FM)
+        mm1(1, 1, PLANES)
         turn_h(0, 2, 1)
         turn_h(0, 3)
-        mm1(1, 2, FM + 1)
+        mm1(1, 2, PLANES + 1)
         scale_out(2, 0)
         turn_x(2, 1)
         tanh(1, 0)
         mm1(1, 3)
-        for j in range(TILES):
-            stats(0, j)
-        for j in range(TILES):
-            moments(0, j)
-        inv_root(0)
+        statistics(0, range(TILES))
         scale_out(2, 1)
         tanh(1, 1)
         late_bias()
         tanh(1, 2)
-        for i in range(3, nch):
-            c_cast, c_scale, c_tanh, c_stat, c_norm, c_late, c_quant = range(i + 1, i - 6, -1)
-            fill = c_quant < 0
-            on(load, i + 3)
-            if fill:
-                shift(c_norm)
-            turn_x(c_scale, 0)
-            if fill:
-                if c_late < 0:
-                    tanh(c_stat, 3)
-                normalise(c_norm, 3, S)
-                quant_x(c_tanh)
-                on(affine, c_late, 3, 0, V)
-                on(affine, c_late, 3, 1, V)
-                normalise(c_norm, 2, S)
-            else:
-                affine(c_late, 3, 0, S)
-                affine(c_late, 3, 1, S)
-                quant_y(c_quant)
-                mm2(c_quant, FM)
-                shift(c_norm)
-                quant_x(c_tanh)
-            if c_late < 0:
-                late_weights_quantised()
-                cast(c_cast, 1, G, c_tanh)
-                cast(c_cast + 1, 0, G)
-                cast(c_cast + 1, 1, G)
-            on(weave, c_late, 0, N, G)
-            if not fill:
-                tanh(c_stat, 3)
-                normalise(c_norm, 3, S)
-                normalise(c_norm, 2, S, 384, H)
-            normalise(c_norm, 0, V)
-            normalise(c_norm, 1, V)
-            on(finish, c_quant)
-            mm1(c_tanh, 0)
-            if not fill:
-                on(cast, c_cast, 0, S)
-            if not fill:
-                normalise(c_norm, 2, V, 0, 384)
-            order = (3, 2, 0, 1) if fill else (0, 3, 1, 2)
-            turn_h(c_stat, order[0], 1 if fill else 2)
-            turn_h(c_stat, order[1], 0)
-            if fill:
-                turn_z(c_norm, 0, 0)
-            turn_h(c_stat, order[2], 0)
-            if not fill:
-                turn_z(c_norm, 0, 0)
-            tanh(c_tanh, 0)
-            mm1(c_tanh, 1)
-            turn_h(c_stat, order[3], 1)
-            if not fill:
-                on(cast, c_cast, 1, S)
-            scale_out(c_scale, 0)
-            turn_z(c_norm, 1, 1)
-            turn_x(c_scale, 1)
-            affine(c_norm, 0, 0, S)
-            affine(c_norm, 0, 1, S)
+
+        def end_of_step(c_scale, c_tanh, c_stat, c_norm, order):
+            affines(c_norm, 0, S)
             tanh(c_tanh, 1)
             mm1(c_tanh, 2)
             turn_z(c_norm, 2, 1)
-            for j in order:
-                stats(c_stat, j)
-            for j in order:
-                moments(c_stat, j)
-            inv_root(c_stat)
+            statistics(c_stat, order)
             scale_out(c_scale, 1)
-            affine(c_norm, 1, 0, S)
-            affine(c_norm, 1, 1, S)
+            affines(c_norm, 1, S)
             turn_z(c_norm, 3, 2)
             tanh(c_tanh, 2)
             mm1(c_tanh, 3)
-            affine(c_norm, 2, 0, S)
-            affine(c_norm, 2, 1, S)
-            if c_late < 0:
+            affines(c_norm, 2, S)
+
+        for c_scale in (3, 4):
+            c_tanh, c_stat, c_norm = c_scale - 1, c_scale - 2, c_scale - 3
+            load(c_scale + 3)
+            shift(c_norm)
+            turn_x(c_scale, 0)
+            if c_norm == 0:
+                tanh(c_stat, 3)
+            normalise(c_norm, 3, S)
+            quant_x(c_tanh)
+            if c_norm == 0:
+                normalise(c_norm, 2, S)
+                late_weights_quantised()
+                cast(4, 1, G, c_tanh)
+                cast(5, 0, G)
+                cast(5, 1, G)
+            else:
+                affines(0, 3, V)
+                normalise(c_norm, 2, S)
+                weave(0, 0, N, G)
+            normalise(c_norm, 0, V)
+            normalise(c_norm, 1, V)
+            mm1(c_tanh, 0)
+            turn_h(c_stat, 3, 1)
+            turn_h(c_stat, 2)
+            turn_z(c_norm, 0)
+            turn_h(c_stat, 0)
+            tanh(c_tanh, 0)
+            mm1(c_tanh, 1)
+            turn_h(c_stat, 1, 1)
+            scale_out(c_scale, 0)
+            turn_z(c_norm, 1, 1)
+            turn_x(c_scale, 1)
+            end_of_step(c_scale, c_tanh, c_stat, c_norm, (3, 2, 0, 1))
+            if c_norm == 0:
                 tanh(c_tanh, 3)
 
-        b, c, d, e, f = range(nch - 5, nch)
-        affine(c, 3, 0, S)
-        affine(c, 3, 1, S)
+        for c_scale in range(5, CHUNKS):
+            c_cast = c_scale + 1
+            c_tanh, c_stat, c_norm, c_weave, c_out = range(c_scale - 1, c_scale - 6, -1)
+            if c_scale + 3 < CHUNKS:
+                load(c_scale + 3)
+            turn_x(c_scale, 0)
+            affines(c_weave, 3, S)
+            quant_y(c_out)
+            mm2(c_out, PLANES)
+            shift(c_norm)
+            quant_x(c_tanh)
+            weave(c_weave, 0, N, G)
+            tanh(c_stat, 3)
+            normalise(c_norm, 3, S)
+            normalise(c_norm, 2, S, NORMALISE_ON_VECTOR, H)
+            normalise(c_norm, 0, V)
+            normalise(c_norm, 1, V)
+            finish(c_out)
+            mm1(c_tanh, 0)
+            if c_cast < CHUNKS:
+                cast(c_cast, 0, S)
+            normalise(c_norm, 2, V, 0, NORMALISE_ON_VECTOR)
+            turn_h(c_stat, 0, 2)
+            turn_h(c_stat, 3)
+            turn_h(c_stat, 1)
+            turn_z(c_norm, 0)
+            tanh(c_tanh, 0)
+            mm1(c_tanh, 1)
+            turn_h(c_stat, 2, 1)
+            if c_cast < CHUNKS:
+                cast(c_cast, 1, S)
+            scale_out(c_scale, 0)
+            turn_z(c_norm, 1, 1)
+            turn_x(c_scale, 1)
+            end_of_step(c_scale, c_tanh, c_stat, c_norm, (0, 3, 1, 2))
+
+        b, c, d, e, f = range(CHUNKS - 5, CHUNKS)
+        affines(c, 3, S)
         quant_y(b)
         mm2(b)
         shift(d)
         quant_x(f)
-        weave(c, 0, 416, G)
+        weave(c, 0, WEAVE_SHORT, G)
         tanh(e, 3)
         normalise(d, 0, V)
         normalise(d, 1, V)
@@ -451,7 +451,7 @@ def tile_rnnclassifier_pa_t_kernel(tc, h1_bytes, h1_scale, W_ih1, b_ih1, b_hh1, 
         finish(b)
         normalise(d, 3, S)
         normalise(d, 2, S)
-        mm1(f, 1, X)
+        mm1(f, 1, WORDS)
         turn_h(e, 3)
         turn_h(e, 2)
         turn_z(d, 0)
@@ -459,84 +459,64 @@ def tile_rnnclassifier_pa_t_kernel(tc, h1_bytes, h1_scale, W_ih1, b_ih1, b_hh1, 
         mm1(f, 2)
         turn_z(d, 1, 1)
         tanh(f, 1)
-        mm1(f, 3, X)
-        for j in (0, 1, 3, 2):
-            stats(e, j)
-        affine(d, 0, 0, S)
-        affine(d, 0, 1, S)
+        mm1(f, 3, WORDS)
+        affines(d, 0, S)
         turn_z(d, 2, 1)
         tanh(f, 2)
         tanh(f, 3)
-        for j in (0, 1, 3, 2):
-            moments(e, j)
-        inv_root(e)
-        affine(d, 1, 0, V)
-        affine(d, 1, 1, V)
+        statistics(e, (0, 1, 3, 2))
+        affines(d, 1, V)
         turn_z(d, 3, 2)
-        affine(d, 2, 0, S)
-        affine(d, 2, 1, S)
+        affines(d, 2, S)
 
         shift(e)
         normalise(e, 0, V)
         turn_h(f, 0, 2)
-        weave(c, 416, N, V)
+        weave(c, WEAVE_SHORT, N, V)
         normalise(e, 2, S)
         normalise(e, 3, S)
         normalise(e, 1, V)
-        turn_h(f, 2, 0)
+        turn_h(f, 2)
         turn_z(e, 0)
         turn_h(f, 1)
         quant_y(c)
-        affine(d, 3, 0, S)
-        affine(d, 3, 1, S)
-        weave(d, 0, 256, G)
+        affines(d, 3, S)
+        weave(d, 0, N // 2, G)
         turn_h(f, 3, 1)
         turn_z(e, 1)
         mm2(c)
-        turn_z(e, 2, 1, S1)
-        for j in (0, 2, 1, 3):
-            stats(f, j)
-        affine(e, 0, 0, S)
-        affine(e, 0, 1, S)
-        turn_z(e, 3, 1, FM)
-        for j in (0, 2, 1, 3):
-            moments(f, j)
-        inv_root(f)
+        turn_z(e, 2, 1, FIRST)
+        affines(e, 0, S)
+        turn_z(e, 3, 1, PLANES)
+        statistics(f, (0, 2, 1, 3))
         finish(c)
-        affine(e, 3, 0, V)
-        for t in (1, 2):
-            affine(e, t, 0, S)
-            affine(e, t, 1, S)
-        affine(e, 3, 1, V)
+        affines(e, 3, V)
+        affines(e, 1, S)
+        affines(e, 2, S)
 
-        weave(d, 256, N, G)
-        weave(e, 0, 256, S)
-        normalise(f, 0, V)
-        normalise(f, 1, V)
-        for t in range(T):
-            turn_z("a", t, 0, (X, HT, HT + 1, FM + 1)[t])
-        normalise(f, 2, V)
-        normalise(f, 3, V)
-        for t in range(T):
-            turn_z("b", t, 0, (S1, HT + 2, HT + 3, FM)[t])
+        weave(d, N // 2, N, G)
+        weave(e, 0, N // 2, S)
+        for u, banks in (("a", (WORDS, HELD, HELD + 1, PLANES + 1)), ("b", (FIRST, HELD + 2, HELD + 3, PLANES))):
+            for j in range(tiles(u)[1], tiles(u)[1] + 2):
+                normalise(f, j, V)
+            for t in range(T):
+                turn_z(u, t, 0, banks[t])
         quant_y(d)
         for t in range(T):
-            affine("a", t, 0, S)
-            affine("a", t, 1, S)
-        mm2(d, X)
-        weave(e, 256, N, V)
+            affines("a", t, S)
+        mm2(d)
+        weave(e, N // 2, N, V)
         quant_y(e)
-        mm2(e, HT)
+        mm2(e, HELD)
         finish(d)
         for t in range(T):
-            affine("b", t, 0, S)
-            affine("b", t, 1, S)
+            affines("b", t, S)
         weave("b", 0, N // 2, S)
         weave("a", 0, N // 2, V)
         finish(e)
         quant_y("a")
-        mm2("a", HT + 1)
+        mm2("a", HELD + 1)
         quant_y("b")
-        mm2("b", FM + 1)
+        mm2("b", PLANES + 1)
         finish("a")
         finish("b")

@@ -25,7 +25,7 @@ WORDS, FIRST, PLANES, HELD = 0, 1, 2, 4
 
 HALVES = {"a": (CHUNKS - 1, 0, 2), "b": (CHUNKS - 1, 2, 2)}
 
-NORMALISE_ON_VECTOR = 256
+NORMALISE_ON_VECTOR = 128
 WEAVE_SHORT = 416
 
 

from contextlib import ExitStack

import concourse.mybir as mybir
from concourse.masks import make_identity

B, H, H2, D_OUT = 8192, 512, 1024, 128
P = 128
T = 4
TILES = 4
N = TILES * P
CHUNKS = B // N
EPS = 1e-5
FLOPS = 2 * B * H * H + 2 * B * H2 * D_OUT

F32 = mybir.dt.float32
BF16 = mybir.dt.bfloat16
U32 = mybir.dt.uint32
U8 = mybir.dt.uint8
FP8 = mybir.dt.float8_e4m3fn
FP8X4 = mybir.dt.float8_e4m3fn_x4
ACT = mybir.ActivationFunctionType
ALU = mybir.AluOpType

WORDS, FIRST, PLANES, HELD = 0, 1, 2, 4

HALVES = {"a": (CHUNKS - 1, 0, 2), "b": (CHUNKS - 1, 2, 2)}

NORMALISE_ON_VECTOR = 128
WEAVE_SHORT = 416


def tile_rnnclassifier_pa_t_kernel(tc, h1_bytes, h1_scale, W_ih1, b_ih1, b_hh1, ln_g, ln_b, fc_W, fc_b, out):
    nc = tc.nc
    V, S, G = nc.vector, nc.scalar, nc.gpsimd

    def rows(ap, c):
        return ap[c * N : (c + 1) * N, :].rearrange("(q j) k -> q j k", j=TILES)

    with ExitStack() as ctx:
        const = ctx.enter_context(tc.tile_pool(name="const", bufs=1))
        work = ctx.enter_context(tc.tile_pool(name="work", bufs=2))
        stat = ctx.enter_context(tc.tile_pool(name="stat", bufs=3))
        psum = ctx.enter_context(tc.psum_pool(name="psum", bufs=1))
        ctx.enter_context(tc.manual_schedule())

        xb, hx, xg, xc, xs = {}, {}, {}, {}, {}
        hh, ht, zz, mv, rs, nm = {}, {}, {}, {}, {}, {}
        yy, yg, yc, ys = {}, {}, {}, {}
        fmb, xtb, s1b, ob = {}, {}, {}, {}

        def load(c, h=None):
            j0, m = (0, TILES) if h is None else (2 * h, 2)
            raw = work.tile([P, m * H], U8, name="x_bytes", align_bytes=64, bufs=6)
            nc.sync.dma_start(out=raw[:].rearrange("p (j k) -> p j k", k=H), in_=rows(h1_bytes, c)[:, j0 : j0 + m, :])
            for g in range(m // 2):
                xb[c, j0 // 2 + g] = raw[:, 2 * g * H : 2 * (g + 1) * H]

        ident = const.tile([P, P], F32, name="ident")
        make_identity(nc, ident[:])
        half = const.tile([P, TILES], F32, name="half")
        nc.gpsimd.memset(half[:], -0.5)

        sums = const.tile([P, TILES, 9], F32, name="sums")
        nc.gpsimd.memset(sums[:], 0.0)
        nc.gpsimd.tensor_scalar(out=sums[:, :, 8], in0=sums[:, :, 8], scalar1=0.0, scalar2=EPS * H, op0=ALU.mult, op1=ALU.add)

        w_sb = {}

        def load_w(h):
            w_sb[h] = const.tile([P, 2, H], BF16, name="w_sb%d" % h)
            nc.sync.dma_start(out=w_sb[h][:], in_=W_ih1.rearrange("(m t) k -> m t k", t=T)[:, 2 * h : 2 * h + 2, :])

        load(0, 0)
        load_w(0)
        load(0, 1)
        load_w(1)
        s4 = const.tile([P, T], F32, name="s4")
        nc.sync.dma_start(out=s4[:], in_=h1_scale.rearrange("o (p t) -> p (o t)", t=T))
        load(1)
        bi_raw = const.tile([P, T], BF16, name="bi_raw")
        nc.sync.dma_start(out=bi_raw[:], in_=b_ih1.rearrange("(p t) -> p t", t=T))
        bh_raw = const.tile([P, T], BF16, name="bh_raw")
        nc.sync.dma_start(out=bh_raw[:], in_=b_hh1.rearrange("(p t) -> p t", t=T))
        load(2)
        load(3)
        f_sb = const.tile([P, H2], BF16, name="f_sb")
        nc.sync.dma_start(out=f_sb[:], in_=fc_W)
        g_raw = const.tile([P, 2, T], BF16, name="g_raw")
        nc.sync.dma_start(out=g_raw[:], in_=ln_g.rearrange("(o p t) -> p o t", o=2, t=T))
        b_raw = const.tile([P, 2, T], BF16, name="b_raw")
        nc.sync.dma_start(out=b_raw[:], in_=ln_b.rearrange("(o p t) -> p o t", o=2, t=T))
        fb_raw = const.tile([P, 1], BF16, name="fb_raw")
        nc.sync.dma_start(out=fb_raw[:], in_=fc_b.rearrange("(p o) -> p o", o=1))
        fb_col = const.tile([P, 1], F32, name="fb_col")
        bias = const.tile([P, T], F32, name="bias")
        g_col = const.tile([P, 2, T], F32, name="g_col")
        b_col = const.tile([P, 2, T], F32, name="b_col")
        fcb = const.tile([P, D_OUT], F32, name="fcb")

        w_grp = const.tile([P, H, T], BF16, align_bytes=64, name="w_grp")
        w_codes = const.tile([P, H], U32, align_bytes=64, name="w_codes")
        w_scales = const.tile([P, H], U8, align_bytes=64, name="w_scales")
        f_grp = const.tile([P, 2 * D_OUT, T], BF16, align_bytes=64, name="f_grp")
        f_codes = const.tile([P, 2 * D_OUT], U32, align_bytes=64, name="f_codes")
        f_scales = const.tile([P, 2 * D_OUT], U8, align_bytes=64, name="f_scales")

        def words(ap):
            return ap.bitcast(F32)

        def cast(c, h, eng, after=None):
            if after is None:
                hx[c, h] = work.tile([P, 2 * H], BF16, name="hx", align_bytes=64, bufs=8)
            else:
                hx[c, h] = work.tile([P, 2 * H], BF16, name="xg%d" % (after % 3), align_bytes=64, bufs=1)
            if eng is S:
                nc.scalar.copy(out=hx[c, h][:], in_=xb[c, h].bitcast(FP8))
            else:
                eng.tensor_copy(out=hx[c, h][:], in_=xb[c, h].bitcast(FP8))

        def bank(k, shape):
            return psum.tile(shape, F32, name="bank%d" % k)

        def turn_x(c, h, k=WORDS):
            xtb[c, h] = bank(k, [P, 2, 2 * P])
            for jj in range(2):
                w = words(hx[c, h][:, jj * H : (jj + 1) * H])
                for u in range(2):
                    nc.tensor.transpose(xtb[c, h][:, u, jj * P : (jj + 1) * P], w[:, u : H // 2 : 2], ident[:])

        def scale_out(c, h):
            if c not in xg:
                xg[c] = work.tile([P, N, T], BF16, name="xg%d" % (c % 3), align_bytes=64, bufs=1)
            n = 2 * P
            nc.vector.tensor_tensor(
                out=xg[c][:, h * n : (h + 1) * n, :].rearrange("p n (u e) -> p n u e", e=2),
                in0=xtb[c, h][:].bitcast(BF16).rearrange("p u (n e) -> p n u e", e=2),
                in1=s4[:].rearrange("p (u e) -> p u e", e=2).unsqueeze(1).to_broadcast([P, n, 2, 2]),
                op=ALU.mult,
            )

        def quant_x(c):
            xc[c] = work.tile([P, N], U32, name="xc", align_bytes=64)
            xs[c] = work.tile([P, N], U8, name="xs", align_bytes=64)
            nc.vector.quantize_mx(out=xc[c][:].bitcast(FP8X4), scales=xs[c][:], in_=xg[c][:].rearrange("p n t -> p (n t)"))

        def mm1(c, t, k=FIRST):
            s1b[c, t] = bank(k, [P, N])
            nc.tensor.matmul_mx(
                out=s1b[c, t][:],
                lhsT=w_codes[:, t * P : (t + 1) * P].bitcast(FP8X4),
                lhsT_scale=w_scales[:, t * P : (t + 1) * P],
                rhs=xc[c][:].bitcast(FP8X4),
                rhs_scale=xs[c][:],
                start=True,
                stop=True,
            )

        def tanh(c, t):
            hh[c, t] = work.tile([P, N], F32, name="hh", bufs=2 * T)
            nc.scalar.activation(out=hh[c, t][:], in_=s1b[c, t][:], func=ACT.Tanh, bias=bias[:, t : t + 1])

        def turn(dst, src, plain):
            if plain:
                nc.tensor.matmul(dst, lhsT=src, rhs=ident[:], start=True, stop=True)
            else:
                nc.tensor.transpose(dst, src, ident[:])

        def turn_h(c, j, plain=0):
            ht[c, j] = bank(HELD + j, [P, H])
            for t in range(T):
                turn(ht[c, j][:, t * P : (t + 1) * P], hh[c, t][:, j * P : (j + 1) * P], t < plain)

        def stats(c, j):
            nc.vector.bn_stats(out=sums[:, j, 0:6], in_=ht[c, j][:])

        def moments(c, j):
            if c not in mv:
                mv[c] = stat.tile([P, TILES, 2], F32, name="mv")
            nc.vector.bn_aggr(out=mv[c][:, j, :], in_=sums[:, j, :])

        def inv_root(c):
            rs[c] = stat.tile([P, TILES], F32, name="rs")
            nc.gpsimd.tensor_tensor(out=rs[c][:], in0=mv[c][:, :, 1], in1=half[:], op=ALU.pow)

        def shift(c):
            nm[c] = stat.tile([P, TILES], F32, name="nm")
            nc.vector.scalar_tensor_tensor(out=nm[c][:], in0=mv[c][:, :, 0], scalar=-1.0, in1=rs[c][:], op0=ALU.mult, op1=ALU.mult)

        def normalise(c, j, eng, lo=0, hi=H):
            if (c, j) not in zz:
                zz[c, j] = work.tile([P, H], F32, name="zz", bufs=2 * TILES)
            rstd = rs[c][:, j : j + 1]
            if eng is V:
                nc.vector.tensor_scalar(out=zz[c, j][:, lo:hi], in0=ht[c, j][:, lo:hi], scalar1=mv[c][:, j, 0:1], scalar2=rstd, op0=ALU.subtract, op1=ALU.mult)
            else:
                nc.scalar.activation(out=zz[c, j][:, lo:hi], in_=ht[c, j][:, lo:hi], func=ACT.Identity, scale=rstd, bias=nm[c][:, j : j + 1])

        def tiles(u):
            return HALVES.get(u, (u, 0, TILES))

        def turn_z(u, t, plain=0, k=None):
            c, j0, m = tiles(u)
            fmb[u, t] = bank(PLANES + t % 2 if k is None else k, [P, m * P])
            for j in range(m):
                turn(fmb[u, t][:, j * P : (j + 1) * P], zz[c, j0 + j][:, t * P : (t + 1) * P], j < plain)

        def affine(u, t, o, eng):
            if u not in yy:
                yy[u] = work.tile([P, 2, T, tiles(u)[2] * P], BF16, name="yy", bufs=3)
            gain, offset = g_col[:, o, t : t + 1], b_col[:, o, t : t + 1]
            if eng is V:
                nc.vector.tensor_scalar(out=yy[u][:, o, t, :], in0=fmb[u, t][:], scalar1=gain, scalar2=offset, op0=ALU.mult, op1=ALU.add)
            else:
                nc.scalar.activation(out=yy[u][:, o, t, :], in_=fmb[u, t][:], func=ACT.Identity, scale=gain, bias=offset)

        def weave(u, lo, hi, eng):
            if u not in yg:
                tag = "yg_%s" % u if u in HALVES or u == CHUNKS - 2 else "yg"
                yg[u] = work.tile([P, 2, tiles(u)[2] * P, T], BF16, name=tag, align_bytes=64, bufs=1)
            dst, src = yg[u][:, :, lo:hi, :], yy[u][:, :, :, lo:hi]
            if eng is G:
                nc.gpsimd.tensor_scalar(out=dst, in0=src.rearrange("p o t n -> p o n t"), scalar1=1.0, scalar2=0.0, op0=ALU.mult, op1=ALU.add)
            elif eng is V:
                nc.vector.tensor_copy(out=dst.rearrange("p o (n i) t -> p o n t i", i=4), in_=src.rearrange("p o t (n i) -> p o n t i", i=4))
            else:
                for o in range(2):
                    nc.scalar.copy(out=dst[:, o].rearrange("p (n i) t -> p n t i", i=4), in_=src[:, o].rearrange("p t (n i) -> p n t i", i=4))

        def quant_y(u):
            n = tiles(u)[2] * P
            yc[u] = work.tile([P, 2 * n], U32, name="yc", align_bytes=64)
            ys[u] = work.tile([P, 2 * n], U8, name="ys", align_bytes=64)
            nc.vector.quantize_mx(out=yc[u][:].bitcast(FP8X4), scales=ys[u][:], in_=yg[u][:].rearrange("p o n t -> p (o n t)"))

        def mm2(u, k=WORDS):
            m = tiles(u)[2]
            ob[u] = bank(k, [P, m, D_OUT])
            for j in range(m):
                for o in range(2):
                    cols = slice((o * m + j) * P, (o * m + j + 1) * P)
                    nc.tensor.matmul_mx(
                        out=ob[u][:, j, :],
                        lhsT=yc[u][:, cols].bitcast(FP8X4),
                        lhsT_scale=ys[u][:, cols],
                        rhs=f_codes[:, o * P : (o + 1) * P].bitcast(FP8X4),
                        rhs_scale=f_scales[:, o * P : (o + 1) * P],
                        start=(o == 0),
                        stop=(o == 1),
                    )

        def finish(u):
            c, j0, m = tiles(u)
            osb = work.tile([P, m, D_OUT], F32, name="osb", bufs=3)
            nc.vector.tensor_tensor(out=osb[:], in0=ob[u][:], in1=fcb[:].unsqueeze(1).to_broadcast([P, m, D_OUT]), op=ALU.add)
            nc.sync.dma_start(out=rows(out, c)[:, j0 : j0 + m, :], in_=osb[:])

        def turn_weights(pieces, grp, k):
            xt = bank(k, [P, 4 * P])
            v = xt[:].rearrange("p (a u r) -> p a u r", a=2, u=2)
            for a in range(2):
                for u in range(2):
                    nc.tensor.transpose(v[:, a, u, :], pieces[a][:, u : H // 2 : 2], ident[:])
            nc.scalar.copy(out=words(grp).rearrange("p (j r) u -> p j r u", j=2), in_=v.rearrange("p j u r -> p j r u"))

        def first_weights(h):
            turn_weights([words(w_sb[h][:, a, :]) for a in range(2)], w_grp[:, h * 2 * P : (h + 1) * 2 * P, :], PLANES + h)

        def first_bias():
            nc.gpsimd.tensor_tensor(out=bias[:], in0=bi_raw[:], in1=bh_raw[:], op=ALU.add)

        def first_weights_quantised(h):
            cols = slice(h * 2 * P, (h + 1) * 2 * P)
            nc.vector.quantize_mx(out=w_codes[:, cols].bitcast(FP8X4), scales=w_scales[:, cols], in_=w_grp[:, cols, :].rearrange("p n t -> p (n t)"))

        def late_constants():
            nc.gpsimd.tensor_copy(out=g_col[:], in_=g_raw[:])
            nc.gpsimd.tensor_copy(out=b_col[:], in_=b_raw[:])
            nc.gpsimd.tensor_copy(out=fb_col[:], in_=fb_raw[:])

        def late_bias():
            fk = bank(PLANES, [P, D_OUT])
            nc.tensor.transpose(fk[:], fb_col[:].to_broadcast([P, P]), ident[:])
            nc.scalar.copy(out=fcb[:], in_=fk[:])

        def late_weights():
            fw = words(f_sb[:])
            turn_weights([fw[:, o * H // 2 : (o + 1) * H // 2] for o in range(2)], f_grp[:], HELD + 2)

        def late_weights_quantised():
            nc.vector.quantize_mx(out=f_codes[:].bitcast(FP8X4), scales=f_scales[:], in_=f_grp[:].rearrange("p n t -> p (n t)"))

        def affines(u, t, eng):
            for o in range(2):
                affine(u, t, o, eng)

        def statistics(c, order):
            for j in order:
                stats(c, j)
            for j in order:
                moments(c, j)
            inv_root(c)

        cast(0, 0, V)
        turn_x(0, 0)
        cast(0, 1, S)
        turn_x(0, 1, HELD)
        first_weights(0)
        cast(1, 1, S)
        first_weights(1)
        first_bias()
        cast(1, 0, G)
        scale_out(0, 0)
        scale_out(0, 1)
        turn_x(1, 0)
        turn_x(1, 1, HELD + 1)
        first_weights_quantised(0)
        quant_x(0)
        first_weights_quantised(1)
        for t, k in enumerate((FIRST, PLANES, PLANES + 1, HELD + 3)):
            mm1(0, t, k)
        cast(2, 0, S)
        scale_out(1, 0)
        turn_x(2, 0)
        scale_out(1, 1)
        late_constants()
        cast(2, 1, G)
        for t in range(T):
            tanh(0, t)
        late_weights()
        quant_x(1)
        load(4)
        load(5)
        cast(3, 0, G, 1)
        cast(3, 1, G)
        cast(4, 0, G)
        turn_h(0, 0)
        turn_h(0, 1)
        mm1(1, 0)
        mm1(1, 1, PLANES)
        turn_h(0, 2, 1)
        turn_h(0, 3)
        mm1(1, 2, PLANES + 1)
        scale_out(2, 0)
        turn_x(2, 1)
        tanh(1, 0)
        mm1(1, 3)
        statistics(0, range(TILES))
        scale_out(2, 1)
        tanh(1, 1)
        late_bias()
        tanh(1, 2)

        def end_of_step(c_scale, c_tanh, c_stat, c_norm, order):
            affines(c_norm, 0, S)
            tanh(c_tanh, 1)
            mm1(c_tanh, 2)
            turn_z(c_norm, 2, 1)
            statistics(c_stat, order)
            scale_out(c_scale, 1)
            affines(c_norm, 1, S)
            turn_z(c_norm, 3, 2)
            tanh(c_tanh, 2)
            mm1(c_tanh, 3)
            affines(c_norm, 2, S)

        for c_scale in (3, 4):
            c_tanh, c_stat, c_norm = c_scale - 1, c_scale - 2, c_scale - 3
            load(c_scale + 3)
            shift(c_norm)
            turn_x(c_scale, 0)
            if c_norm == 0:
                tanh(c_stat, 3)
            normalise(c_norm, 3, S)
            quant_x(c_tanh)
            if c_norm == 0:
                normalise(c_norm, 2, S)
                late_weights_quantised()
                cast(4, 1, G, c_tanh)
                cast(5, 0, G)
                cast(5, 1, G)
            else:
                affines(0, 3, V)
                normalise(c_norm, 2, S)
                weave(0, 0, N, G)
            normalise(c_norm, 0, V)
            normalise(c_norm, 1, V)
            mm1(c_tanh, 0)
            turn_h(c_stat, 3, 1)
            turn_h(c_stat, 2)
            turn_z(c_norm, 0)
            turn_h(c_stat, 0)
            tanh(c_tanh, 0)
            mm1(c_tanh, 1)
            turn_h(c_stat, 1, 1)
            scale_out(c_scale, 0)
            turn_z(c_norm, 1, 1)
            turn_x(c_scale, 1)
            end_of_step(c_scale, c_tanh, c_stat, c_norm, (3, 2, 0, 1))
            if c_norm == 0:
                tanh(c_tanh, 3)

        for c_scale in range(5, CHUNKS):
            c_cast = c_scale + 1
            c_tanh, c_stat, c_norm, c_weave, c_out = range(c_scale - 1, c_scale - 6, -1)
            if c_scale + 3 < CHUNKS:
                load(c_scale + 3)
            turn_x(c_scale, 0)
            affines(c_weave, 3, S)
            quant_y(c_out)
            mm2(c_out, PLANES)
            shift(c_norm)
            quant_x(c_tanh)
            weave(c_weave, 0, N, G)
            tanh(c_stat, 3)
            normalise(c_norm, 3, S)
            normalise(c_norm, 2, S, NORMALISE_ON_VECTOR, H)
            normalise(c_norm, 0, V)
            normalise(c_norm, 1, V)
            finish(c_out)
            mm1(c_tanh, 0)
            if c_cast < CHUNKS:
                cast(c_cast, 0, S)
            normalise(c_norm, 2, V, 0, NORMALISE_ON_VECTOR)
            turn_h(c_stat, 0, 2)
            turn_h(c_stat, 3)
            turn_h(c_stat, 1)
            turn_z(c_norm, 0)
            tanh(c_tanh, 0)
            mm1(c_tanh, 1)
            turn_h(c_stat, 2, 1)
            if c_cast < CHUNKS:
                cast(c_cast, 1, S)
            scale_out(c_scale, 0)
            turn_z(c_norm, 1, 1)
            turn_x(c_scale, 1)
            end_of_step(c_scale, c_tanh, c_stat, c_norm, (0, 3, 1, 2))

        b, c, d, e, f = range(CHUNKS - 5, CHUNKS)
        affines(c, 3, S)
        quant_y(b)
        mm2(b)
        shift(d)
        quant_x(f)
        weave(c, 0, WEAVE_SHORT, G)
        tanh(e, 3)
        normalise(d, 0, V)
        normalise(d, 1, V)
        turn_h(e, 0)
        mm1(f, 0)
        turn_h(e, 1)
        finish(b)
        normalise(d, 3, S)
        normalise(d, 2, S)
        mm1(f, 1, WORDS)
        turn_h(e, 3)
        turn_h(e, 2)
        turn_z(d, 0)
        tanh(f, 0)
        mm1(f, 2)
        turn_z(d, 1, 1)
        tanh(f, 1)
        mm1(f, 3, WORDS)
        affines(d, 0, S)
        turn_z(d, 2, 1)
        tanh(f, 2)
        tanh(f, 3)
        statistics(e, (0, 1, 3, 2))
        affines(d, 1, V)
        turn_z(d, 3, 2)
        affines(d, 2, S)

        shift(e)
        normalise(e, 0, V)
        turn_h(f, 0, 2)
        weave(c, WEAVE_SHORT, N, V)
        normalise(e, 2, S)
        normalise(e, 3, S)
        normalise(e, 1, V)
        turn_h(f, 2)
        turn_z(e, 0)
        turn_h(f, 1)
        quant_y(c)
        affines(d, 3, S)
        weave(d, 0, N // 2, G)
        turn_h(f, 3, 1)
        turn_z(e, 1)
        mm2(c)
        turn_z(e, 2, 1, FIRST)
        affines(e, 0, S)
        turn_z(e, 3, 1, PLANES)
        statistics(f, (0, 2, 1, 3))
        finish(c)
        affines(e, 3, V)
        affines(e, 1, S)
        affines(e, 2, S)

        weave(d, N // 2, N, G)
        weave(e, 0, N // 2, S)
        for u, banks in (("a", (WORDS, HELD, HELD + 1, PLANES + 1)), ("b", (FIRST, HELD + 2, HELD + 3, PLANES))):
            for j in range(tiles(u)[1], tiles(u)[1] + 2):
                normalise(f, j, V)
            for t in range(T):
                turn_z(u, t, 0, banks[t])
        quant_y(d)
        for t in range(T):
            affines("a", t, S)
        mm2(d)
        weave(e, N // 2, N, V)
        quant_y(e)
        mm2(e, HELD)
        finish(d)
        for t in range(T):
            affines("b", t, S)
        weave("b", 0, N // 2, S)
        weave("a", 0, N // 2, V)
        finish(e)
        quant_y("a")
        mm2("a", HELD + 1)
        quant_y("b")
        mm2("b", PLANES + 1)
        finish("a")
        finish("b")
